import numpy as np
import ml_dtypes


def mxq(x, axis, fmt="e4m3"):
    dtype, down = {"e4m3": (ml_dtypes.float8_e4m3fn, 7), "e5m2": (ml_dtypes.float8_e5m2, 14)}[fmt]
    v = np.moveaxis(np.asarray(x, np.float32).astype(ml_dtypes.bfloat16).astype(np.float64), axis, -1)
    blocks = v.reshape(v.shape[:-1] + (-1, 32))
    amax = np.abs(blocks).max(-1, keepdims=True)
    byte = np.maximum(np.where(amax > 0, np.frexp(amax)[1] - 1 + 127, 0) - down, 1)
    scale = np.exp2(byte - 127.0)
    codes = (blocks / scale).astype(np.float32).astype(dtype).astype(np.float64)
    return np.moveaxis((codes * scale).reshape(v.shape), -1, axis)


WIDE = False


def mx_kscale(k):
    if not WIDE:
        return np.ones(k)
    levels = np.array([30, -30])
    if k % 512:
        return np.exp2(np.random.permutation(np.resize(levels, k // 32))).repeat(32)
    a = np.empty((k // 512, 16))
    for p in range(k // 512):
        a[p, :8] = np.random.permutation(np.resize(levels, 8))
        for g in range(8):
            far = levels[np.abs(levels - a[p, g]) >= 10]
            a[p, g + 8] = far[np.random.randint(len(far))]
    return np.exp2(a.ravel()).repeat(32)


BF16 = ml_dtypes.bfloat16


def bf(x):
    return np.asarray(x, np.float32).astype(BF16)


def f64(x):
    return np.asarray(x).astype(np.float64)


B, S, D, H = 4, 1024, 512, 4
DH = D // H
ROPE_BASE = 10000.0


def rope_split(x, freqs_cis):
    b, s, h, dh = x.shape
    xr = x.reshape(b, s, h, dh // 2, 2)
    x_real, x_imag = xr[..., 0], xr[..., 1]
    fc = freqs_cis[:s][:, None, :, :]
    cos, sin = fc[..., 0], fc[..., 1]
    rot_real = x_real * cos - x_imag * sin
    rot_imag = x_real * sin + x_imag * cos
    return np.concatenate([rot_real, rot_imag], axis=-1)


def setup_inputs():
    s = mx_kscale(D)
    inv_freq = 1.0 / ROPE_BASE ** (np.arange(0, DH, 2) / DH)
    ang = np.outer(np.arange(S), inv_freq)
    return {"hidden_states": bf(np.random.standard_normal((B, S, D)) * s),
            "freqs_cis": bf(np.stack([np.cos(ang), np.sin(ang)], axis=-1)),
            "Wq": bf(np.random.standard_normal((D, D)) / np.sqrt(D) / s),
            "bq": bf(np.random.standard_normal(D) * 0.3),
            "Wk": bf(np.random.standard_normal((D, D)) / np.sqrt(D) / s),
            "bk": bf(np.random.standard_normal(D) * 0.3)}


def reference(hidden_states, freqs_cis, Wq, bq, Wk, bk):
    x = f64(hidden_states)
    b, s, _ = x.shape
    fc = f64(freqs_cis)
    xq = mxq(x, 2, "e5m2")
    q = ((xq @ mxq(f64(Wq), 1, "e5m2").T) + f64(bq)).reshape(b, s, H, DH)
    k = ((xq @ mxq(f64(Wk), 1, "e5m2").T) + f64(bk)).reshape(b, s, H, DH)
    return rope_split(q, fc), rope_split(k, fc)

@@ -1,0 +1,241 @@
+from contextlib import ExitStack
+
+import concourse.mybir as mybir
+from concourse.masks import make_identity
+
+F32 = mybir.dt.float32
+BF16 = mybir.dt.bfloat16
+U32 = mybir.dt.uint32
+U8 = mybir.dt.uint8
+FP8X4 = mybir.dt.float8_e5m2_x4
+ADD = mybir.AluOpType.add
+MULT = mybir.AluOpType.mult
+
+P = 128
+D = 512
+TOKENS = 4096
+GROUP = 512
+N_GROUPS = TOKENS // GROUP
+N_STEPS = 2 * N_GROUPS
+
+FLOPS = 2 * TOKENS * D * 2 * D
+
+
+def tile_attention_pa_t_kernel(tc, hidden_states, freqs_cis, Wq, bq, Wk, bk, out_0, out_1):
+    nc = tc.nc
+    x_rows = hidden_states.rearrange("b s k -> (b s) k")
+    out_rows = (
+        out_0.rearrange("b s h d -> (b s) (h d)"),
+        out_1.rearrange("b s h d -> (b s) (h d)"),
+    )
+    w_dram = (Wq, Wk)
+    b_dram = (bq, bk)
+
+    with ExitStack() as ctx:
+        const = ctx.enter_context(tc.tile_pool(name="const", bufs=1))
+        work = ctx.enter_context(tc.tile_pool(name="work", bufs=2))
+        psum = ctx.enter_context(tc.psum_pool(name="psum", bufs=1))
+
+        w_raw = [const.tile([P, 2, 2, D], BF16, name="w_raw%d" % qk) for qk in range(2)]
+        b_raw = [const.tile([P, 2, 2], BF16, name="b_raw%d" % qk) for qk in range(2)]
+        x_raw = [const.tile([P, 4, D], BF16, name="x_raw%d" % g) for g in range(N_GROUPS)]
+        f_raw = const.tile([P, 2, 4, P], BF16, name="f_raw")
+        f_dup = const.tile([P, 8, 2, 64], F32, name="f_dup")
+        cs_tab = const.tile([P, 2, 2, GROUP], BF16, name="cs_tab")
+        nsc_tab = const.tile([P, 2, 2, GROUP], BF16, name="nsc_tab")
+        w_grouped = [const.tile([P, 4 * D], BF16, name="w_grouped%d" % qk, align_bytes=64) for qk in range(2)]
+        w_codes = const.tile([P, 2 * D], U32, name="w_codes", align_bytes=64)
+        w_scales = const.tile([P, 2 * D], U8, name="w_scales", align_bytes=64)
+        bias_f = const.tile([P, 8], F32, name="bias_f")
+        ident = const.tile([P, P], F32, name="ident")
+        warm_in = const.tile([P, 1], F32, name="warm_in")
+        warm_out = const.tile([P, 1], F32, name="warm_out")
+
+        def load_w(qk, hh):
+            nc.sync.dma_start(
+                out=w_raw[qk][:, hh],
+                in_=w_dram[qk].rearrange("(hh m eo) k -> m hh eo k", hh=2, eo=2)[:, hh],
+            )
+
+        def load_x(g):
+            nc.sync.dma_start(
+                out=x_raw[g][:],
+                in_=x_rows[g * GROUP : (g + 1) * GROUP, :].rearrange("(p n) k -> p n k", n=4),
+            )
+
+        f_view = freqs_cis.rearrange("(hf p n) j c -> p hf n (j c)", hf=2, n=4)
+
+        with nc.allow_non_contiguous_dma(reason="each bias is 1 KiB, laid one feature pair to a partition"):
+            for qk in range(2):
+                nc.scalar.dma_start(
+                    out=b_raw[qk][:],
+                    in_=b_dram[qk].rearrange("(hh m eo) -> m hh eo", hh=2, eo=2),
+                )
+        load_w(0, 0)
+        load_x(0)
+        nc.sync.dma_start(out=f_raw[:, 0], in_=f_view[:, 0])
+        load_w(0, 1)
+        load_w(1, 0)
+        load_w(1, 1)
+        load_x(1)
+        nc.sync.dma_start(out=f_raw[:, 1], in_=f_view[:, 1])
+        for g in range(2, N_GROUPS):
+            load_x(g)
+
+        nc.vector.memset(warm_in[:], 0.0)
+        nc.scalar.copy(out=warm_out[:], in_=warm_in[:])
+        make_identity(nc, ident[:])
+
+        def k_to_partitions(rows_pair, grouped_words, copy):
+            tp = psum.tile([P, 2, 2, P], F32, tag="tp", bufs=3, name="tp")
+            for i in range(2):
+                words = rows_pair[i].bitcast(F32)
+                for u in range(2):
+                    nc.tensor.transpose(tp[:, u, i, :], words[:, u : D // 2 : 2], ident[:])
+            copy(out=grouped_words, in_=tp[:].rearrange("p u i r -> p (i r) u"))
+
+        def prep_w(qk, hh, copy):
+            words = w_grouped[qk][:].bitcast(F32).rearrange("p (c u) -> p c u", u=2)
+            k_to_partitions(
+                (w_raw[qk][:, hh, 0, :], w_raw[qk][:, hh, 1, :]),
+                words[:, hh * 256 : (hh + 1) * 256, :],
+                copy,
+            )
+
+        def quant_w(qk, hh):
+            c0 = qk * D + hh * 256
+            nc.vector.quantize_mx(
+                out=w_codes[:, c0 : c0 + 256].bitcast(FP8X4),
+                scales=w_scales[:, c0 : c0 + 256],
+                in_=w_grouped[qk][:, hh * 1024 : (hh + 1) * 1024],
+            )
+
+        x_grouped = {}
+        x_codes = {}
+        x_scales = {}
+
+        def prep_x(g):
+            xg = work.tile([P, 4 * GROUP], BF16, tag="xg", bufs=2, name="xg", align_bytes=64)
+            x_grouped[g] = xg
+            words = xg[:].bitcast(F32).rearrange("p (c u) -> p c u", u=2)
+            for hf in range(2):
+                k_to_partitions(
+                    (x_raw[g][:, 2 * hf, :], x_raw[g][:, 2 * hf + 1, :]),
+                    words[:, hf * 256 : (hf + 1) * 256, :],
+                    nc.scalar.copy,
+                )
+
+        def quant_x(g):
+            xc = work.tile([P, GROUP], U32, tag="xc", bufs=3, name="xc", align_bytes=64)
+            xs = work.tile([P, GROUP], U8, tag="xs", bufs=3, name="xs", align_bytes=64)
+            x_codes[g] = xc
+            x_scales[g] = xs
+            nc.vector.quantize_mx(out=xc[:].bitcast(FP8X4), scales=xs[:], in_=x_grouped[g][:])
+
+        def prep_tables(hf):
+            words = f_raw[:, hf].bitcast(F32)
+            for a in range(2):
+                nc.vector.tensor_copy(out=f_dup[:, hf * 4 : (hf + 1) * 4, a, :], in_=words)
+            tp = psum.tile([P, 4, P], F32, tag="tp", bufs=3, name="tpf")
+            for n in range(4):
+                nc.tensor.transpose(tp[:, n, :], f_dup[:, hf * 4 + n].rearrange("p a j -> p (a j)"), ident[:])
+            halves = tp[:].rearrange("p n r -> p (n r)").bitcast(BF16).rearrange("p (t c) -> p c t", c=2)
+            nc.scalar.copy(out=cs_tab[:, hf], in_=halves)
+            nc.vector.tensor_scalar_mul(out=nsc_tab[:, hf, 0, :], in0=halves[:, 1, :], scalar1=-1.0)
+            nc.vector.tensor_copy(out=nsc_tab[:, hf, 1, :], in_=halves[:, 0, :])
+
+        acc = {}
+        prod = {}
+        sums = {}
+
+        def mx(t):
+            g, qk = divmod(t, 2)
+            for i in range(4):
+                w = qk * 4 + i
+                a = psum.tile([P, GROUP], F32, tag="mx", bufs=5, name="acc")
+                acc[(t, i)] = a
+                nc.tensor.matmul_mx(
+                    out=a[:],
+                    lhsT=w_codes[:, w * P : (w + 1) * P].bitcast(FP8X4),
+                    lhsT_scale=w_scales[:, w * P : (w + 1) * P],
+                    rhs=x_codes[g][:].bitcast(FP8X4),
+                    rhs_scale=x_scales[g][:],
+                    start=True,
+                    stop=True,
+                )
+
+        def mult(t):
+            g, qk = divmod(t, 2)
+            hf = g % 2
+            for i in range(4):
+                w = qk * 4 + i
+                table = cs_tab if i % 2 == 0 else nsc_tab
+                pr = work.tile([P, 2, GROUP], F32, tag="prod", bufs=10, name="pr")
+                prod[(t, i)] = pr
+                nc.vector.scalar_tensor_tensor(
+                    out=pr[:],
+                    in0=acc[(t, i)][:].unsqueeze(1).to_broadcast([P, 2, GROUP]),
+                    scalar=bias_f[:, w : w + 1],
+                    in1=table[:, hf],
+                    op0=ADD,
+                    op1=MULT,
+                )
+
+        def add(t):
+            sm = work.tile([P, 2, GROUP], F32, tag="sm", bufs=3, name="sm")
+            sums[t] = sm
+            nc.gpsimd.tensor_tensor(out=sm[:], in0=prod[(t, 0)][:], in1=prod[(t, 1)][:], op=ADD)
+
+        def back(t):
+            g, qk = divmod(t, 2)
+            o = work.tile([P, 4, D], F32, tag="o", bufs=3, name="o")
+            dst_rows = out_rows[qk][g * GROUP : (g + 1) * GROUP, :].rearrange("(p n) f -> p n f", n=4)
+            for n in range(4):
+                cols = slice(n * P, (n + 1) * P)
+                bt = psum.tile([P, D], F32, tag="tp", bufs=3, name="bt")
+                for ri in range(2):
+                    nc.tensor.transpose(bt[:, ri * 256 : ri * 256 + P], sums[t][:, ri, cols], ident[:])
+                    dst = bt[:, ri * 256 + P : ri * 256 + 2 * P]
+                    nc.tensor.matmul(
+                        out=dst, lhsT=prod[(t, 2)][:, ri, cols], rhs=ident[:], is_transpose=True, start=True, stop=False
+                    )
+                    nc.tensor.matmul(
+                        out=dst, lhsT=prod[(t, 3)][:, ri, cols], rhs=ident[:], is_transpose=True, start=False, stop=True
+                    )
+                nc.scalar.copy(
+                    out=o[:, n, :].rearrange("p (h ri j) -> p h ri j", h=4, ri=2),
+                    in_=bt[:].rearrange("p (ri h j) -> p h ri j", ri=2, h=4),
+                )
+                if n % 2 == 1:
+                    nc.sync.dma_start(out=dst_rows[:, n - 1 : n + 1, :], in_=o[:, n - 1 : n + 1, :])
+
+        prep_w(0, 0, nc.vector.tensor_copy)
+        prep_x(0)
+        quant_w(0, 0)
+        prep_tables(0)
+        quant_x(0)
+        prep_w(0, 1, nc.vector.tensor_copy)
+        for qk in range(2):
+            nc.vector.tensor_copy(
+                out=bias_f[:, qk * 4 : (qk + 1) * 4], in_=b_raw[qk][:].rearrange("p hh eo -> p (hh eo)")
+            )
+        quant_w(0, 1)
+
+        for t in range(N_STEPS):
+            g, qk = divmod(t, 2)
+            if qk == 1 and g + 1 < N_GROUPS:
+                quant_x(g + 1)
+            mx(t)
+            mult(t)
+            add(t)
+            if t == 0:
+                prep_w(1, 0, nc.scalar.copy)
+                prep_w(1, 1, nc.scalar.copy)
+                quant_w(1, 0)
+                quant_w(1, 1)
+                prep_tables(1)
+            if qk == 0 and g + 1 < N_GROUPS:
+                prep_x(g + 1)
+            if t >= 1:
+                back(t - 1)
+        back(N_STEPS - 1)

@@ -10,6 +10,7 @@ U8 = mybir.dt.uint8
 FP8X4 = mybir.dt.float8_e5m2_x4
 ADD = mybir.AluOpType.add
 MULT = mybir.AluOpType.mult
+IDENTITY = mybir.ActivationFunctionType.Identity
 
 P = 128
 D = 512
@@ -17,6 +18,8 @@ TOKENS = 4096
 GROUP = 512
 N_GROUPS = TOKENS // GROUP
 N_STEPS = 2 * N_GROUPS
+G_SUM_RI = (0,)
+WARM_UP = 12
 
 FLOPS = 2 * TOKENS * D * 2 * D
 
@@ -35,6 +38,7 @@ def tile_attention_pa_t_kernel(tc, hidden_states, freqs_cis, Wq, bq, Wk, bk, out
         const = ctx.enter_context(tc.tile_pool(name="const", bufs=1))
         work = ctx.enter_context(tc.tile_pool(name="work", bufs=2))
         psum = ctx.enter_context(tc.psum_pool(name="psum", bufs=1))
+        ctx.enter_context(tc.manual_schedule())
 
         w_raw = [const.tile([P, 2, 2, D], BF16, name="w_raw%d" % qk) for qk in range(2)]
         b_raw = [const.tile([P, 2, 2], BF16, name="b_raw%d" % qk) for qk in range(2)]
@@ -57,10 +61,10 @@ def tile_attention_pa_t_kernel(tc, hidden_states, freqs_cis, Wq, bq, Wk, bk, out
                 in_=w_dram[qk].rearrange("(hh m eo) k -> m hh eo k", hh=2, eo=2)[:, hh],
             )
 
-        def load_x(g):
+        def load_x(g, n0, n1):
             nc.sync.dma_start(
-                out=x_raw[g][:],
-                in_=x_rows[g * GROUP : (g + 1) * GROUP, :].rearrange("(p n) k -> p n k", n=4),
+                out=x_raw[g][:, n0:n1, :],
+                in_=x_rows[g * GROUP : (g + 1) * GROUP, :].rearrange("(p n) k -> p n k", n=4)[:, n0:n1, :],
             )
 
         f_view = freqs_cis.rearrange("(hf p n) j c -> p hf n (j c)", hf=2, n=4)
@@ -71,59 +75,63 @@ def tile_attention_pa_t_kernel(tc, hidden_states, freqs_cis, Wq, bq, Wk, bk, out
                     out=b_raw[qk][:],
                     in_=b_dram[qk].rearrange("(hh m eo) -> m hh eo", hh=2, eo=2),
                 )
+        load_x(0, 0, 2)
         load_w(0, 0)
-        load_x(0)
-        nc.sync.dma_start(out=f_raw[:, 0], in_=f_view[:, 0])
+        load_x(0, 2, 4)
         load_w(0, 1)
+        nc.sync.dma_start(out=f_raw[:, 0], in_=f_view[:, 0])
         load_w(1, 0)
         load_w(1, 1)
-        load_x(1)
+        load_x(1, 0, 4)
         nc.sync.dma_start(out=f_raw[:, 1], in_=f_view[:, 1])
         for g in range(2, N_GROUPS):
-            load_x(g)
+            load_x(g, 0, 4)
 
         nc.vector.memset(warm_in[:], 0.0)
         nc.scalar.copy(out=warm_out[:], in_=warm_in[:])
         make_identity(nc, ident[:])
+        if WARM_UP > 0:
+            wu = psum.tile([P, 4, P], F32, tag="tp", bufs=3, name="wu")
+            for i in range(WARM_UP):
+                nc.tensor.transpose(wu[:, i % 4, :], ident[:], ident[:])
 
-        def k_to_partitions(rows_pair, grouped_words, copy):
+        def k_transposes(rows_pair):
             tp = psum.tile([P, 2, 2, P], F32, tag="tp", bufs=3, name="tp")
             for i in range(2):
                 words = rows_pair[i].bitcast(F32)
                 for u in range(2):
                     nc.tensor.transpose(tp[:, u, i, :], words[:, u : D // 2 : 2], ident[:])
+            return tp
+
+        def k_copy(tp, grouped_words, copy):
             copy(out=grouped_words, in_=tp[:].rearrange("p u i r -> p (i r) u"))
 
-        def prep_w(qk, hh, copy):
-            words = w_grouped[qk][:].bitcast(F32).rearrange("p (c u) -> p c u", u=2)
-            k_to_partitions(
-                (w_raw[qk][:, hh, 0, :], w_raw[qk][:, hh, 1, :]),
-                words[:, hh * 256 : (hh + 1) * 256, :],
-                copy,
-            )
+        def w_transposes(qk, hh):
+            return k_transposes((w_raw[qk][:, hh, 0, :], w_raw[qk][:, hh, 1, :]))
 
-        def quant_w(qk, hh):
-            c0 = qk * D + hh * 256
+        def w_copy(tp, qk, hh, copy):
+            words = w_grouped[qk][:].bitcast(F32).rearrange("p (c u) -> p c u", u=2)
+            k_copy(tp, words[:, hh * 256 : (hh + 1) * 256, :], copy)
+
+        def quant_w(qk, hh0, hh1):
             nc.vector.quantize_mx(
-                out=w_codes[:, c0 : c0 + 256].bitcast(FP8X4),
-                scales=w_scales[:, c0 : c0 + 256],
-                in_=w_grouped[qk][:, hh * 1024 : (hh + 1) * 1024],
+                out=w_codes[:, qk * D + hh0 * 256 : qk * D + hh1 * 256].bitcast(FP8X4),
+                scales=w_scales[:, qk * D + hh0 * 256 : qk * D + hh1 * 256],
+                in_=w_grouped[qk][:, hh0 * 1024 : hh1 * 1024],
             )
 
         x_grouped = {}
         x_codes = {}
         x_scales = {}
 
-        def prep_x(g):
-            xg = work.tile([P, 4 * GROUP], BF16, tag="xg", bufs=2, name="xg", align_bytes=64)
-            x_grouped[g] = xg
-            words = xg[:].bitcast(F32).rearrange("p (c u) -> p c u", u=2)
-            for hf in range(2):
-                k_to_partitions(
-                    (x_raw[g][:, 2 * hf, :], x_raw[g][:, 2 * hf + 1, :]),
-                    words[:, hf * 256 : (hf + 1) * 256, :],
-                    nc.scalar.copy,
-                )
+        def fx(f):
+            g, hf = divmod(f, 2)
+            if hf == 0:
+                xg = work.tile([P, 4 * GROUP], BF16, tag="xg", bufs=2, name="xg", align_bytes=64)
+                x_grouped[g] = xg
+            words = x_grouped[g][:].bitcast(F32).rearrange("p (c u) -> p c u", u=2)
+            tp = k_transposes((x_raw[g][:, 2 * hf, :], x_raw[g][:, 2 * hf + 1, :]))
+            k_copy(tp, words[:, hf * 256 : (hf + 1) * 256, :], nc.scalar.copy)
 
         def quant_x(g):
             xc = work.tile([P, GROUP], U32, tag="xc", bufs=3, name="xc", align_bytes=64)
@@ -132,110 +140,170 @@ def tile_attention_pa_t_kernel(tc, hidden_states, freqs_cis, Wq, bq, Wk, bk, out
             x_scales[g] = xs
             nc.vector.quantize_mx(out=xc[:].bitcast(FP8X4), scales=xs[:], in_=x_grouped[g][:])
 
-        def prep_tables(hf):
+        def table_dup(hf):
             words = f_raw[:, hf].bitcast(F32)
             for a in range(2):
                 nc.vector.tensor_copy(out=f_dup[:, hf * 4 : (hf + 1) * 4, a, :], in_=words)
+
+        def table_make(hf):
             tp = psum.tile([P, 4, P], F32, tag="tp", bufs=3, name="tpf")
             for n in range(4):
                 nc.tensor.transpose(tp[:, n, :], f_dup[:, hf * 4 + n].rearrange("p a j -> p (a j)"), ident[:])
             halves = tp[:].rearrange("p n r -> p (n r)").bitcast(BF16).rearrange("p (t c) -> p c t", c=2)
             nc.scalar.copy(out=cs_tab[:, hf], in_=halves)
-            nc.vector.tensor_scalar_mul(out=nsc_tab[:, hf, 0, :], in0=halves[:, 1, :], scalar1=-1.0)
-            nc.vector.tensor_copy(out=nsc_tab[:, hf, 1, :], in_=halves[:, 0, :])
+            nc.gpsimd.tensor_scalar(
+                out=nsc_tab[:, hf, 0, :], in0=cs_tab[:, hf, 1, :], scalar1=-1.0, scalar2=0.0, op0=MULT, op1=ADD
+            )
+            nc.gpsimd.tensor_scalar(
+                out=nsc_tab[:, hf, 1, :], in0=cs_tab[:, hf, 0, :], scalar1=1.0, scalar2=0.0, op0=MULT, op1=ADD
+            )
 
         acc = {}
         prod = {}
         sums = {}
 
-        def mx(t):
+        def mx(t, i):
             g, qk = divmod(t, 2)
-            for i in range(4):
-                w = qk * 4 + i
-                a = psum.tile([P, GROUP], F32, tag="mx", bufs=5, name="acc")
-                acc[(t, i)] = a
-                nc.tensor.matmul_mx(
-                    out=a[:],
-                    lhsT=w_codes[:, w * P : (w + 1) * P].bitcast(FP8X4),
-                    lhsT_scale=w_scales[:, w * P : (w + 1) * P],
-                    rhs=x_codes[g][:].bitcast(FP8X4),
-                    rhs_scale=x_scales[g][:],
-                    start=True,
-                    stop=True,
-                )
+            w = qk * 4 + i
+            a = psum.tile([P, GROUP], F32, tag="mx", bufs=5, name="acc")
+            acc[(t, i)] = a
+            nc.tensor.matmul_mx(
+                out=a[:],
+                lhsT=w_codes[:, w * P : (w + 1) * P].bitcast(FP8X4),
+                lhsT_scale=w_scales[:, w * P : (w + 1) * P],
+                rhs=x_codes[g][:].bitcast(FP8X4),
+                rhs_scale=x_scales[g][:],
+                start=True,
+                stop=True,
+            )
 
-        def mult(t):
+        def vmult(t, i):
             g, qk = divmod(t, 2)
-            hf = g % 2
-            for i in range(4):
-                w = qk * 4 + i
-                table = cs_tab if i % 2 == 0 else nsc_tab
-                pr = work.tile([P, 2, GROUP], F32, tag="prod", bufs=10, name="pr")
-                prod[(t, i)] = pr
-                nc.vector.scalar_tensor_tensor(
-                    out=pr[:],
-                    in0=acc[(t, i)][:].unsqueeze(1).to_broadcast([P, 2, GROUP]),
-                    scalar=bias_f[:, w : w + 1],
-                    in1=table[:, hf],
-                    op0=ADD,
-                    op1=MULT,
-                )
+            w = qk * 4 + i
+            table = cs_tab if i % 2 == 0 else nsc_tab
+            pr = work.tile([P, 2, GROUP], F32, tag="prv", bufs=8, name="prv")
+            prod[(t, i)] = pr
+            nc.vector.scalar_tensor_tensor(
+                out=pr[:],
+                in0=acc[(t, i)][:].unsqueeze(1).to_broadcast([P, 2, GROUP]),
+                scalar=bias_f[:, w : w + 1],
+                in1=table[:, g % 2],
+                op0=ADD,
+                op1=MULT,
+            )
 
-        def add(t):
-            sm = work.tile([P, 2, GROUP], F32, tag="sm", bufs=3, name="sm")
-            sums[t] = sm
-            nc.gpsimd.tensor_tensor(out=sm[:], in0=prod[(t, 0)][:], in1=prod[(t, 1)][:], op=ADD)
-
-        def back(t):
+        def side_mult(t):
             g, qk = divmod(t, 2)
-            o = work.tile([P, 4, D], F32, tag="o", bufs=3, name="o")
+            w = qk * 4 + 3
+            ob = work.tile([P, GROUP], F32, tag="ob", bufs=2, name="ob")
+            nc.scalar.activation(out=ob[:], in_=acc[(t, 3)][:], func=IDENTITY, bias=bias_f[:, w : w + 1], scale=1.0)
+            pr = work.tile([P, 2, GROUP], F32, tag="prg", bufs=4, name="prg")
+            prod[(t, 3)] = pr
+            for c in range(2):
+                nc.gpsimd.tensor_tensor(out=pr[:, c, :], in0=ob[:], in1=nsc_tab[:, g % 2, c, :], op=MULT)
+
+        def gsum(t):
+            for ri in G_SUM_RI:
+                sm = work.tile([P, GROUP], F32, tag="sm", bufs=2 * len(G_SUM_RI) + 1, name="sm")
+                sums[(t, 0, ri)] = sm
+                nc.gpsimd.tensor_tensor(out=sm[:], in0=prod[(t, 0)][:, ri, :], in1=prod[(t, 1)][:, ri, :], op=ADD)
+
+        outs = {}
+
+        def back(t, n_list):
+            g, qk = divmod(t, 2)
+            if t not in outs:
+                o_new = work.tile([P, 4, D], F32, tag="o", bufs=3, name="o")
+                outs[t] = o_new
+            o = outs[t]
             dst_rows = out_rows[qk][g * GROUP : (g + 1) * GROUP, :].rearrange("(p n) f -> p n f", n=4)
-            for n in range(4):
+            for n in n_list:
                 cols = slice(n * P, (n + 1) * P)
                 bt = psum.tile([P, D], F32, tag="tp", bufs=3, name="bt")
-                for ri in range(2):
-                    nc.tensor.transpose(bt[:, ri * 256 : ri * 256 + P], sums[t][:, ri, cols], ident[:])
-                    dst = bt[:, ri * 256 + P : ri * 256 + 2 * P]
-                    nc.tensor.matmul(
-                        out=dst, lhsT=prod[(t, 2)][:, ri, cols], rhs=ident[:], is_transpose=True, start=True, stop=False
-                    )
-                    nc.tensor.matmul(
-                        out=dst, lhsT=prod[(t, 3)][:, ri, cols], rhs=ident[:], is_transpose=True, start=False, stop=True
-                    )
+                for hh in range(2):
+                    for ri in range(2):
+                        dst = bt[:, ri * 256 + hh * P : ri * 256 + (hh + 1) * P]
+                        if (t, hh, ri) in sums:
+                            nc.tensor.transpose(dst, sums[(t, hh, ri)][:, cols], ident[:])
+                        else:
+                            nc.tensor.matmul(
+                                out=dst,
+                                lhsT=prod[(t, 2 * hh)][:, ri, cols],
+                                rhs=ident[:],
+                                is_transpose=True,
+                                start=True,
+                                stop=False,
+                            )
+                            nc.tensor.matmul(
+                                out=dst,
+                                lhsT=prod[(t, 2 * hh + 1)][:, ri, cols],
+                                rhs=ident[:],
+                                is_transpose=True,
+                                start=False,
+                                stop=True,
+                            )
                 nc.scalar.copy(
                     out=o[:, n, :].rearrange("p (h ri j) -> p h ri j", h=4, ri=2),
                     in_=bt[:].rearrange("p (ri h j) -> p h ri j", ri=2, h=4),
                 )
-                if n % 2 == 1:
-                    nc.sync.dma_start(out=dst_rows[:, n - 1 : n + 1, :], in_=o[:, n - 1 : n + 1, :])
+            n0 = n_list[0]
+            n1 = n_list[-1] + 1
+            nc.sync.dma_start(out=dst_rows[:, n0:n1, :], in_=o[:, n0:n1, :])
 
-        prep_w(0, 0, nc.vector.tensor_copy)
-        prep_x(0)
-        quant_w(0, 0)
-        prep_tables(0)
+        def next_banks(t):
+            for i in (3, 0, 1, 2):
+                mx(t, i)
+            side_mult(t)
+
+        fx(0)
+        tp_w = w_transposes(0, 0)
+        w_copy(tp_w, 0, 0, nc.vector.tensor_copy)
+        fx(1)
+        tp_w = w_transposes(0, 1)
+        table_dup(0)
+        quant_w(0, 0, 1)
+        table_make(0)
         quant_x(0)
-        prep_w(0, 1, nc.vector.tensor_copy)
+        w_copy(tp_w, 0, 1, nc.vector.tensor_copy)
         for qk in range(2):
             nc.vector.tensor_copy(
                 out=bias_f[:, qk * 4 : (qk + 1) * 4], in_=b_raw[qk][:].rearrange("p hh eo -> p (hh eo)")
             )
-        quant_w(0, 1)
+        mx(0, 0)
+        mx(0, 1)
+        vmult(0, 0)
+        quant_w(0, 1, 2)
+        for hh in range(2):
+            tp_w = w_transposes(1, hh)
+            w_copy(tp_w, 1, hh, nc.scalar.copy)
+        fx(2)
+        mx(0, 3)
+        mx(0, 2)
+        side_mult(0)
+        vmult(0, 1)
+        gsum(0)
+        quant_w(1, 0, 2)
+        vmult(0, 2)
+        fx(3)
+        next_banks(1)
+        table_dup(1)
+        table_make(1)
+        quant_x(1)
+        fx(4)
 
-        for t in range(N_STEPS):
+        for t in range(1, N_STEPS):
             g, qk = divmod(t, 2)
-            if qk == 1 and g + 1 < N_GROUPS:
-                quant_x(g + 1)
-            mx(t)
-            mult(t)
-            add(t)
-            if t == 0:
-                prep_w(1, 0, nc.scalar.copy)
-                prep_w(1, 1, nc.scalar.copy)
-                quant_w(1, 0)
-                quant_w(1, 1)
-                prep_tables(1)
+            vmult(t, 0)
             if qk == 0 and g + 1 < N_GROUPS:
-                prep_x(g + 1)
-            if t >= 1:
-                back(t - 1)
-        back(N_STEPS - 1)
+                quant_x(g + 1)
+            vmult(t, 1)
+            gsum(t)
+            vmult(t, 2)
+            back(t - 1, (0, 1))
+            if t + 1 < N_STEPS:
+                next_banks(t + 1)
+            back(t - 1, (2, 3))
+            if t + 4 < N_STEPS:
+                fx(t + 4)
+        back(N_STEPS - 1, (0, 1))
+        back(N_STEPS - 1, (2, 3))

@@ -19,7 +19,7 @@ GROUP = 512
 N_GROUPS = TOKENS // GROUP
 N_STEPS = 2 * N_GROUPS
 G_SUM_RI = (0,)
-WARM_UP = 12
+HEAD_DUMMIES = 6
 
 FLOPS = 2 * TOKENS * D * 2 * D
 
@@ -52,6 +52,7 @@ def tile_attention_pa_t_kernel(tc, hidden_states, freqs_cis, Wq, bq, Wk, bk, out
         w_scales = const.tile([P, 2 * D], U8, name="w_scales", align_bytes=64)
         bias_f = const.tile([P, 8], F32, name="bias_f")
         ident = const.tile([P, P], F32, name="ident")
+        zeros = const.tile([P, GROUP], BF16, name="zeros")
         warm_in = const.tile([P, 1], F32, name="warm_in")
         warm_out = const.tile([P, 1], F32, name="warm_out")
 
@@ -87,13 +88,17 @@ def tile_attention_pa_t_kernel(tc, hidden_states, freqs_cis, Wq, bq, Wk, bk, out
         for g in range(2, N_GROUPS):
             load_x(g, 0, 4)
 
+        nc.vector.memset(zeros[:], 0.0)
         nc.vector.memset(warm_in[:], 0.0)
         nc.scalar.copy(out=warm_out[:], in_=warm_in[:])
         make_identity(nc, ident[:])
-        if WARM_UP > 0:
-            wu = psum.tile([P, 4, P], F32, tag="tp", bufs=3, name="wu")
-            for i in range(WARM_UP):
-                nc.tensor.transpose(wu[:, i % 4, :], ident[:], ident[:])
+
+        def dummies(count):
+            scratch = psum.tile([P, GROUP], F32, tag="mx", bufs=5, name="scratch")
+            for i in range(count):
+                nc.tensor.matmul(out=scratch[:], lhsT=zeros[:, 0:P], rhs=zeros[:], start=True, stop=True)
+
+        dummies(HEAD_DUMMIES)
 
         def k_transposes(rows_pair):
             tp = psum.tile([P, 2, 2, P], F32, tag="tp", bufs=3, name="tp")
@@ -177,17 +182,18 @@ def tile_attention_pa_t_kernel(tc, hidden_states, freqs_cis, Wq, bq, Wk, bk, out
                 stop=True,
             )
 
-        def vmult(t, i):
+        def vmult(t, i, c0, c1):
             g, qk = divmod(t, 2)
             w = qk * 4 + i
             table = cs_tab if i % 2 == 0 else nsc_tab
-            pr = work.tile([P, 2, GROUP], F32, tag="prv", bufs=8, name="prv")
-            prod[(t, i)] = pr
+            if (t, i) not in prod:
+                pr_new = work.tile([P, 2, GROUP], F32, tag="prv", bufs=8, name="prv")
+                prod[(t, i)] = pr_new
             nc.vector.scalar_tensor_tensor(
-                out=pr[:],
-                in0=acc[(t, i)][:].unsqueeze(1).to_broadcast([P, 2, GROUP]),
+                out=prod[(t, i)][:, :, c0:c1],
+                in0=acc[(t, i)][:, c0:c1].unsqueeze(1).to_broadcast([P, 2, c1 - c0]),
                 scalar=bias_f[:, w : w + 1],
-                in1=table[:, g % 2],
+                in1=table[:, g % 2, :, c0:c1],
                 op0=ADD,
                 op1=MULT,
             )
@@ -202,11 +208,17 @@ def tile_attention_pa_t_kernel(tc, hidden_states, freqs_cis, Wq, bq, Wk, bk, out
             for c in range(2):
                 nc.gpsimd.tensor_tensor(out=pr[:, c, :], in0=ob[:], in1=nsc_tab[:, g % 2, c, :], op=MULT)
 
-        def gsum(t):
+        def gsum(t, c0, c1):
             for ri in G_SUM_RI:
-                sm = work.tile([P, GROUP], F32, tag="sm", bufs=2 * len(G_SUM_RI) + 1, name="sm")
-                sums[(t, 0, ri)] = sm
-                nc.gpsimd.tensor_tensor(out=sm[:], in0=prod[(t, 0)][:, ri, :], in1=prod[(t, 1)][:, ri, :], op=ADD)
+                if (t, 0, ri) not in sums:
+                    sm_new = work.tile([P, GROUP], F32, tag="sm", bufs=2 * len(G_SUM_RI) + 1, name="sm")
+                    sums[(t, 0, ri)] = sm_new
+                nc.gpsimd.tensor_tensor(
+                    out=sums[(t, 0, ri)][:, c0:c1],
+                    in0=prod[(t, 0)][:, ri, c0:c1],
+                    in1=prod[(t, 1)][:, ri, c0:c1],
+                    op=ADD,
+                )
 
         outs = {}
 
@@ -250,15 +262,12 @@ def tile_attention_pa_t_kernel(tc, hidden_states, freqs_cis, Wq, bq, Wk, bk, out
             n1 = n_list[-1] + 1
             nc.sync.dma_start(out=dst_rows[:, n0:n1, :], in_=o[:, n0:n1, :])
 
-        def next_banks(t):
-            for i in (3, 0, 1, 2):
-                mx(t, i)
-            side_mult(t)
 
         fx(0)
         tp_w = w_transposes(0, 0)
         w_copy(tp_w, 0, 0, nc.vector.tensor_copy)
         fx(1)
+        dummies(2)
         tp_w = w_transposes(0, 1)
         table_dup(0)
         quant_w(0, 0, 1)
@@ -271,7 +280,7 @@ def tile_attention_pa_t_kernel(tc, hidden_states, freqs_cis, Wq, bq, Wk, bk, out
             )
         mx(0, 0)
         mx(0, 1)
-        vmult(0, 0)
+        vmult(0, 0, 0, GROUP)
         quant_w(0, 1, 2)
         for hh in range(2):
             tp_w = w_transposes(1, hh)
@@ -280,30 +289,55 @@ def tile_attention_pa_t_kernel(tc, hidden_states, freqs_cis, Wq, bq, Wk, bk, out
         mx(0, 3)
         mx(0, 2)
         side_mult(0)
-        vmult(0, 1)
-        gsum(0)
+        vmult(0, 1, 0, GROUP)
+        gsum(0, 0, GROUP)
         quant_w(1, 0, 2)
-        vmult(0, 2)
-        fx(3)
-        next_banks(1)
         table_dup(1)
+        vmult(0, 2, 0, GROUP)
+        fx(3)
+        mx(1, 3)
+        mx(1, 0)
+        side_mult(1)
         table_make(1)
         quant_x(1)
         fx(4)
+        mx(1, 1)
+        mx(1, 2)
 
-        for t in range(1, N_STEPS):
+        last = N_STEPS - 1
+        for t in range(1, last):
             g, qk = divmod(t, 2)
-            vmult(t, 0)
+            vmult(t, 0, 0, GROUP)
             if qk == 0 and g + 1 < N_GROUPS:
                 quant_x(g + 1)
-            vmult(t, 1)
-            gsum(t)
-            vmult(t, 2)
+            vmult(t, 1, 0, GROUP)
+            gsum(t, 0, GROUP)
+            vmult(t, 2, 0, GROUP)
             back(t - 1, (0, 1))
-            if t + 1 < N_STEPS:
-                next_banks(t + 1)
+            mx(t + 1, 3)
+            mx(t + 1, 0)
+            side_mult(t + 1)
             back(t - 1, (2, 3))
             if t + 4 < N_STEPS:
                 fx(t + 4)
-        back(N_STEPS - 1, (0, 1))
-        back(N_STEPS - 1, (2, 3))
+            mx(t + 1, 1)
+            mx(t + 1, 2)
+
+        half = GROUP // 2
+        vmult(last, 0, 0, half)
+        vmult(last, 1, 0, half)
+        gsum(last, 0, half)
+        vmult(last, 2, 0, half)
+        back(last - 1, (0, 1))
+        dummies(2)
+        back(last - 1, (2, 3))
+        dummies(2)
+        vmult(last, 0, half, GROUP)
+        vmult(last, 1, half, GROUP)
+        gsum(last, half, GROUP)
+        vmult(last, 2, half, GROUP)
+        back(last, (0,))
+        back(last, (1,))
+        dummies(2)
+        back(last, (2,))
+        back(last, (3,))

@@ -18,8 +18,7 @@ TOKENS = 4096
 GROUP = 512
 N_GROUPS = TOKENS // GROUP
 N_STEPS = 2 * N_GROUPS
-G_SUM_RI = (0,)
-HEAD_DUMMIES = 6
+HEAD_DUMMIES = 4
 
 FLOPS = 2 * TOKENS * D * 2 * D
 
@@ -46,13 +45,14 @@ def tile_attention_pa_t_kernel(tc, hidden_states, freqs_cis, Wq, bq, Wk, bk, out
         f_raw = const.tile([P, 2, 4, P], BF16, name="f_raw")
         f_dup = const.tile([P, 8, 2, 64], F32, name="f_dup")
         cs_tab = const.tile([P, 2, 2, GROUP], BF16, name="cs_tab")
-        nsc_tab = const.tile([P, 2, 2, GROUP], BF16, name="nsc_tab")
+        nsc_tab = const.tile([P, 2, 2, GROUP], F32, name="nsc_tab")
         w_grouped = [const.tile([P, 4 * D], BF16, name="w_grouped%d" % qk, align_bytes=64) for qk in range(2)]
         w_codes = const.tile([P, 2 * D], U32, name="w_codes", align_bytes=64)
         w_scales = const.tile([P, 2 * D], U8, name="w_scales", align_bytes=64)
         bias_f = const.tile([P, 8], F32, name="bias_f")
         ident = const.tile([P, P], F32, name="ident")
         zeros = const.tile([P, GROUP], BF16, name="zeros")
+        zeros32 = const.tile([P, P], F32, name="zeros32")
         warm_in = const.tile([P, 1], F32, name="warm_in")
         warm_out = const.tile([P, 1], F32, name="warm_out")
 
@@ -89,16 +89,19 @@ def tile_attention_pa_t_kernel(tc, hidden_states, freqs_cis, Wq, bq, Wk, bk, out
             load_x(g, 0, 4)
 
         nc.vector.memset(zeros[:], 0.0)
+        nc.vector.memset(zeros32[:], 0.0)
         nc.vector.memset(warm_in[:], 0.0)
         nc.scalar.copy(out=warm_out[:], in_=warm_in[:])
         make_identity(nc, ident[:])
 
-        def dummies(count):
-            scratch = psum.tile([P, GROUP], F32, tag="mx", bufs=5, name="scratch")
-            for i in range(count):
+        def dummies(wide, narrow, tag, bufs):
+            scratch = psum.tile([P, GROUP], F32, tag=tag, bufs=bufs, name="scratch")
+            for i in range(wide):
                 nc.tensor.matmul(out=scratch[:], lhsT=zeros[:, 0:P], rhs=zeros[:], start=True, stop=True)
+            for i in range(narrow):
+                nc.tensor.matmul(out=scratch[:, 0:P], lhsT=zeros32[:], rhs=zeros32[:], start=True, stop=True)
 
-        dummies(HEAD_DUMMIES)
+        dummies(HEAD_DUMMIES, 0, "mx", 5)
 
         def k_transposes(rows_pair):
             tp = psum.tile([P, 2, 2, P], F32, tag="tp", bufs=3, name="tp")
@@ -187,7 +190,7 @@ def tile_attention_pa_t_kernel(tc, hidden_states, freqs_cis, Wq, bq, Wk, bk, out
             w = qk * 4 + i
             table = cs_tab if i % 2 == 0 else nsc_tab
             if (t, i) not in prod:
-                pr_new = work.tile([P, 2, GROUP], F32, tag="prv", bufs=8, name="prv")
+                pr_new = work.tile([P, 2, GROUP], F32, tag="prv", bufs=10, name="prv")
                 prod[(t, i)] = pr_new
             nc.vector.scalar_tensor_tensor(
                 out=prod[(t, i)][:, :, c0:c1],
@@ -203,22 +206,36 @@ def tile_attention_pa_t_kernel(tc, hidden_states, freqs_cis, Wq, bq, Wk, bk, out
             w = qk * 4 + 3
             ob = work.tile([P, GROUP], F32, tag="ob", bufs=2, name="ob")
             nc.scalar.activation(out=ob[:], in_=acc[(t, 3)][:], func=IDENTITY, bias=bias_f[:, w : w + 1], scale=1.0)
-            pr = work.tile([P, 2, GROUP], F32, tag="prg", bufs=4, name="prg")
+            pr = work.tile([P, 2, GROUP], F32, tag="prg", bufs=3, name="prg")
             prod[(t, 3)] = pr
             for c in range(2):
                 nc.gpsimd.tensor_tensor(out=pr[:, c, :], in0=ob[:], in1=nsc_tab[:, g % 2, c, :], op=MULT)
 
-        def gsum(t, c0, c1):
-            for ri in G_SUM_RI:
-                if (t, 0, ri) not in sums:
-                    sm_new = work.tile([P, GROUP], F32, tag="sm", bufs=2 * len(G_SUM_RI) + 1, name="sm")
-                    sums[(t, 0, ri)] = sm_new
-                nc.gpsimd.tensor_tensor(
-                    out=sums[(t, 0, ri)][:, c0:c1],
-                    in0=prod[(t, 0)][:, ri, c0:c1],
-                    in1=prod[(t, 1)][:, ri, c0:c1],
-                    op=ADD,
-                )
+        def gsum(t):
+            for ri in range(2):
+                sm = work.tile([P, GROUP], F32, tag="sm", bufs=5, name="sm")
+                sums[(t, 0, ri)] = sm
+                nc.gpsimd.tensor_tensor(out=sm[:], in0=prod[(t, 0)][:, ri, :], in1=prod[(t, 1)][:, ri, :], op=ADD)
+
+        def side(t):
+            return t % 2 == 1 and t < N_STEPS - 1
+
+        def banks_a(t):
+            if side(t):
+                mx(t, 3)
+                mx(t, 0)
+                side_mult(t)
+            else:
+                mx(t, 0)
+                mx(t, 1)
+
+        def banks_b(t):
+            if side(t):
+                mx(t, 1)
+                mx(t, 2)
+            else:
+                mx(t, 2)
+                mx(t, 3)
 
         outs = {}
 
@@ -267,7 +284,7 @@ def tile_attention_pa_t_kernel(tc, hidden_states, freqs_cis, Wq, bq, Wk, bk, out
         tp_w = w_transposes(0, 0)
         w_copy(tp_w, 0, 0, nc.vector.tensor_copy)
         fx(1)
-        dummies(2)
+        dummies(0, 2, "mx", 5)
         tp_w = w_transposes(0, 1)
         table_dup(0)
         quant_w(0, 0, 1)
@@ -286,58 +303,51 @@ def tile_attention_pa_t_kernel(tc, hidden_states, freqs_cis, Wq, bq, Wk, bk, out
             tp_w = w_transposes(1, hh)
             w_copy(tp_w, 1, hh, nc.scalar.copy)
         fx(2)
-        mx(0, 3)
         mx(0, 2)
-        side_mult(0)
+        mx(0, 3)
         vmult(0, 1, 0, GROUP)
-        gsum(0, 0, GROUP)
+        gsum(0)
         quant_w(1, 0, 2)
         table_dup(1)
         vmult(0, 2, 0, GROUP)
+        vmult(0, 3, 0, GROUP)
         fx(3)
-        mx(1, 3)
-        mx(1, 0)
-        side_mult(1)
+        banks_a(1)
         table_make(1)
         quant_x(1)
         fx(4)
-        mx(1, 1)
-        mx(1, 2)
+        banks_b(1)
 
         last = N_STEPS - 1
         for t in range(1, last):
             g, qk = divmod(t, 2)
             vmult(t, 0, 0, GROUP)
+            vmult(t, 1, 0, GROUP)
+            gsum(t)
+            vmult(t, 2, 0, GROUP)
             if qk == 0 and g + 1 < N_GROUPS:
                 quant_x(g + 1)
-            vmult(t, 1, 0, GROUP)
-            gsum(t, 0, GROUP)
-            vmult(t, 2, 0, GROUP)
-            back(t - 1, (0, 1))
-            mx(t + 1, 3)
-            mx(t + 1, 0)
-            side_mult(t + 1)
-            back(t - 1, (2, 3))
+            if not side(t):
+                vmult(t, 3, 0, GROUP)
             if t + 4 < N_STEPS:
                 fx(t + 4)
-            mx(t + 1, 1)
-            mx(t + 1, 2)
+            dummies(1, 1, "tp", 3)
+            back(t - 1, (0, 1))
+            banks_a(t + 1)
+            back(t - 1, (2, 3))
+            banks_b(t + 1)
 
         half = GROUP // 2
-        vmult(last, 0, 0, half)
-        vmult(last, 1, 0, half)
-        gsum(last, 0, half)
-        vmult(last, 2, 0, half)
+        for i in range(4):
+            vmult(last, i, 0, half)
         back(last - 1, (0, 1))
-        dummies(2)
+        dummies(0, 2, "mx", 5)
         back(last - 1, (2, 3))
-        dummies(2)
-        vmult(last, 0, half, GROUP)
-        vmult(last, 1, half, GROUP)
-        gsum(last, half, GROUP)
-        vmult(last, 2, half, GROUP)
+        dummies(0, 2, "mx", 5)
+        for i in range(4):
+            vmult(last, i, half, GROUP)
         back(last, (0,))
         back(last, (1,))
-        dummies(2)
+        dummies(0, 2, "mx", 5)
         back(last, (2,))
         back(last, (3,))

@@ -52,7 +52,6 @@ def tile_attention_pa_t_kernel(tc, hidden_states, freqs_cis, Wq, bq, Wk, bk, out
         bias_f = const.tile([P, 8], F32, name="bias_f")
         ident = const.tile([P, P], F32, name="ident")
         zeros = const.tile([P, GROUP], BF16, name="zeros")
-        zeros32 = const.tile([P, P], F32, name="zeros32")
         warm_in = const.tile([P, 1], F32, name="warm_in")
         warm_out = const.tile([P, 1], F32, name="warm_out")
 
@@ -89,19 +88,16 @@ def tile_attention_pa_t_kernel(tc, hidden_states, freqs_cis, Wq, bq, Wk, bk, out
             load_x(g, 0, 4)
 
         nc.vector.memset(zeros[:], 0.0)
-        nc.vector.memset(zeros32[:], 0.0)
         nc.vector.memset(warm_in[:], 0.0)
         nc.scalar.copy(out=warm_out[:], in_=warm_in[:])
         make_identity(nc, ident[:])
 
-        def dummies(wide, narrow, tag, bufs):
+        def dummies(count, tag, bufs):
             scratch = psum.tile([P, GROUP], F32, tag=tag, bufs=bufs, name="scratch")
-            for i in range(wide):
+            for i in range(count):
                 nc.tensor.matmul(out=scratch[:], lhsT=zeros[:, 0:P], rhs=zeros[:], start=True, stop=True)
-            for i in range(narrow):
-                nc.tensor.matmul(out=scratch[:, 0:P], lhsT=zeros32[:], rhs=zeros32[:], start=True, stop=True)
 
-        dummies(HEAD_DUMMIES, 0, "mx", 5)
+        dummies(HEAD_DUMMIES, "mx", 5)
 
         def k_transposes(rows_pair):
             tp = psum.tile([P, 2, 2, P], F32, tag="tp", bufs=3, name="tp")
@@ -208,17 +204,17 @@ def tile_attention_pa_t_kernel(tc, hidden_states, freqs_cis, Wq, bq, Wk, bk, out
             nc.scalar.activation(out=ob[:], in_=acc[(t, 3)][:], func=IDENTITY, bias=bias_f[:, w : w + 1], scale=1.0)
             pr = work.tile([P, 2, GROUP], F32, tag="prg", bufs=3, name="prg")
             prod[(t, 3)] = pr
-            for c in range(2):
-                nc.gpsimd.tensor_tensor(out=pr[:, c, :], in0=ob[:], in1=nsc_tab[:, g % 2, c, :], op=MULT)
+            nc.gpsimd.tensor_tensor(
+                out=pr[:], in0=ob[:].unsqueeze(1).to_broadcast([P, 2, GROUP]), in1=nsc_tab[:, g % 2], op=MULT
+            )
 
         def gsum(t):
-            for ri in range(2):
-                sm = work.tile([P, GROUP], F32, tag="sm", bufs=5, name="sm")
-                sums[(t, 0, ri)] = sm
-                nc.gpsimd.tensor_tensor(out=sm[:], in0=prod[(t, 0)][:, ri, :], in1=prod[(t, 1)][:, ri, :], op=ADD)
+            sm = work.tile([P, 2, GROUP], F32, tag="sm", bufs=3, name="sm")
+            sums[t] = sm
+            nc.gpsimd.tensor_tensor(out=sm[:], in0=prod[(t, 0)][:], in1=prod[(t, 1)][:], op=ADD)
 
         def side(t):
-            return t % 2 == 1 and t < N_STEPS - 1
+            return t % 2 == 1 and 3 <= t < N_STEPS - 1
 
         def banks_a(t):
             if side(t):
@@ -252,8 +248,8 @@ def tile_attention_pa_t_kernel(tc, hidden_states, freqs_cis, Wq, bq, Wk, bk, out
                 for hh in range(2):
                     for ri in range(2):
                         dst = bt[:, ri * 256 + hh * P : ri * 256 + (hh + 1) * P]
-                        if (t, hh, ri) in sums:
-                            nc.tensor.transpose(dst, sums[(t, hh, ri)][:, cols], ident[:])
+                        if hh == 0 and t in sums:
+                            nc.tensor.transpose(dst, sums[t][:, ri, cols], ident[:])
                         else:
                             nc.tensor.matmul(
                                 out=dst,
@@ -284,7 +280,6 @@ def tile_attention_pa_t_kernel(tc, hidden_states, freqs_cis, Wq, bq, Wk, bk, out
         tp_w = w_transposes(0, 0)
         w_copy(tp_w, 0, 0, nc.vector.tensor_copy)
         fx(1)
-        dummies(0, 2, "mx", 5)
         tp_w = w_transposes(0, 1)
         table_dup(0)
         quant_w(0, 0, 1)
@@ -323,15 +318,15 @@ def tile_attention_pa_t_kernel(tc, hidden_states, freqs_cis, Wq, bq, Wk, bk, out
             g, qk = divmod(t, 2)
             vmult(t, 0, 0, GROUP)
             vmult(t, 1, 0, GROUP)
-            gsum(t)
-            vmult(t, 2, 0, GROUP)
             if qk == 0 and g + 1 < N_GROUPS:
                 quant_x(g + 1)
+            gsum(t)
+            vmult(t, 2, 0, GROUP)
             if not side(t):
                 vmult(t, 3, 0, GROUP)
             if t + 4 < N_STEPS:
                 fx(t + 4)
-            dummies(1, 1, "tp", 3)
+            dummies(2 - t % 2, "tp", 3)
             back(t - 1, (0, 1))
             banks_a(t + 1)
             back(t - 1, (2, 3))
@@ -341,13 +336,10 @@ def tile_attention_pa_t_kernel(tc, hidden_states, freqs_cis, Wq, bq, Wk, bk, out
         for i in range(4):
             vmult(last, i, 0, half)
         back(last - 1, (0, 1))
-        dummies(0, 2, "mx", 5)
         back(last - 1, (2, 3))
-        dummies(0, 2, "mx", 5)
         for i in range(4):
             vmult(last, i, half, GROUP)
         back(last, (0,))
         back(last, (1,))
-        dummies(0, 2, "mx", 5)
         back(last, (2,))
         back(last, (3,))

@@ -128,13 +128,28 @@ def tile_attention_pa_t_kernel(tc, hidden_states, freqs_cis, Wq, bq, Wk, bk, out
         x_codes = {}
         x_scales = {}
 
+        x_split = {}
+
+        def split_x(g):
+            xs_new = work.tile([P, 4, 2, P], F32, tag="xsp", bufs=3, name="xsp")
+            x_split[g] = xs_new
+            nc.scalar.copy(
+                out=xs_new[:], in_=x_raw[g][:].rearrange("p n k -> p (n k)").bitcast(F32).rearrange("p (n w u) -> p n u w", n=4, u=2)
+            )
+
         def fx(f):
             g, hf = divmod(f, 2)
             if hf == 0:
                 xg = work.tile([P, 4 * GROUP], BF16, tag="xg", bufs=2, name="xg", align_bytes=64)
                 x_grouped[g] = xg
             words = x_grouped[g][:].bitcast(F32).rearrange("p (c u) -> p c u", u=2)
-            tp = k_transposes((x_raw[g][:, 2 * hf, :], x_raw[g][:, 2 * hf + 1, :]))
+            if g in x_split:
+                tp = psum.tile([P, 2, 2, P], F32, tag="tp", bufs=3, name="tp")
+                for i in range(2):
+                    for u in range(2):
+                        nc.tensor.transpose(tp[:, u, i, :], x_split[g][:, 2 * hf + i, u, :], ident[:])
+            else:
+                tp = k_transposes((x_raw[g][:, 2 * hf, :], x_raw[g][:, 2 * hf + 1, :]))
             k_copy(tp, words[:, hf * 256 : (hf + 1) * 256, :], nc.scalar.copy)
 
         def quant_x(g):
@@ -326,6 +341,8 @@ def tile_attention_pa_t_kernel(tc, hidden_states, freqs_cis, Wq, bq, Wk, bk, out
                 vmult(t, 3, 0, GROUP)
             if t + 4 < N_STEPS:
                 fx(t + 4)
+            if t % 2 == 1 and t + 5 < N_STEPS:
+                split_x((t + 5) // 2)
             dummies(2 - t % 2, "tp", 3)
             back(t - 1, (0, 1))
             banks_a(t + 1)

@@ -97,10 +97,10 @@ def tile_attention_pa_t_kernel(tc, hidden_states, freqs_cis, Wq, bq, Wk, bk, out
             for i in range(count):
                 nc.tensor.matmul(out=scratch[:], lhsT=zeros[:, 0:P], rhs=zeros[:], start=True, stop=True)
 
-        dummies(HEAD_DUMMIES, "mx", 5)
+        dummies(HEAD_DUMMIES, "mx", 4)
 
         def k_transposes(rows_pair):
-            tp = psum.tile([P, 2, 2, P], F32, tag="tp", bufs=3, name="tp")
+            tp = psum.tile([P, 2, 2, P], F32, tag="tp", bufs=4, name="tp")
             for i in range(2):
                 words = rows_pair[i].bitcast(F32)
                 for u in range(2):
@@ -144,7 +144,7 @@ def tile_attention_pa_t_kernel(tc, hidden_states, freqs_cis, Wq, bq, Wk, bk, out
                 x_grouped[g] = xg
             words = x_grouped[g][:].bitcast(F32).rearrange("p (c u) -> p c u", u=2)
             if g in x_split:
-                tp = psum.tile([P, 2, 2, P], F32, tag="tp", bufs=3, name="tp")
+                tp = psum.tile([P, 2, 2, P], F32, tag="tp", bufs=4, name="tp")
                 for i in range(2):
                     for u in range(2):
                         nc.tensor.transpose(tp[:, u, i, :], x_split[g][:, 2 * hf + i, u, :], ident[:])
@@ -165,7 +165,7 @@ def tile_attention_pa_t_kernel(tc, hidden_states, freqs_cis, Wq, bq, Wk, bk, out
                 nc.vector.tensor_copy(out=f_dup[:, hf * 4 : (hf + 1) * 4, a, :], in_=words)
 
         def table_make(hf):
-            tp = psum.tile([P, 4, P], F32, tag="tp", bufs=3, name="tpf")
+            tp = psum.tile([P, 4, P], F32, tag="tp", bufs=4, name="tpf")
             for n in range(4):
                 nc.tensor.transpose(tp[:, n, :], f_dup[:, hf * 4 + n].rearrange("p a j -> p (a j)"), ident[:])
             halves = tp[:].rearrange("p n r -> p (n r)").bitcast(BF16).rearrange("p (t c) -> p c t", c=2)
@@ -184,7 +184,7 @@ def tile_attention_pa_t_kernel(tc, hidden_states, freqs_cis, Wq, bq, Wk, bk, out
         def mx(t, i):
             g, qk = divmod(t, 2)
             w = qk * 4 + i
-            a = psum.tile([P, GROUP], F32, tag="mx", bufs=5, name="acc")
+            a = psum.tile([P, GROUP], F32, tag="mx", bufs=4, name="acc")
             acc[(t, i)] = a
             nc.tensor.matmul_mx(
                 out=a[:],
@@ -259,7 +259,7 @@ def tile_attention_pa_t_kernel(tc, hidden_states, freqs_cis, Wq, bq, Wk, bk, out
             dst_rows = out_rows[qk][g * GROUP : (g + 1) * GROUP, :].rearrange("(p n) f -> p n f", n=4)
             for n in n_list:
                 cols = slice(n * P, (n + 1) * P)
-                bt = psum.tile([P, D], F32, tag="tp", bufs=3, name="bt")
+                bt = psum.tile([P, D], F32, tag="tp", bufs=4, name="bt")
                 for hh in range(2):
                     for ri in range(2):
                         dst = bt[:, ri * 256 + hh * P : ri * 256 + (hh + 1) * P]
@@ -343,7 +343,7 @@ def tile_attention_pa_t_kernel(tc, hidden_states, freqs_cis, Wq, bq, Wk, bk, out
                 fx(t + 4)
             if t % 2 == 1 and t + 5 < N_STEPS:
                 split_x((t + 5) // 2)
-            dummies(2 - t % 2, "tp", 3)
+            dummies(2 - t % 2, "tp", 4)
             back(t - 1, (0, 1))
             banks_a(t + 1)
             back(t - 1, (2, 3))

@@ -343,7 +343,7 @@ def tile_attention_pa_t_kernel(tc, hidden_states, freqs_cis, Wq, bq, Wk, bk, out
                 fx(t + 4)
             if t % 2 == 1 and t + 5 < N_STEPS:
                 split_x((t + 5) // 2)
-            dummies(2 - t % 2, "tp", 4)
+            dummies(1, "tp", 4)
             back(t - 1, (0, 1))
             banks_a(t + 1)
             back(t - 1, (2, 3))

@@ -313,12 +313,13 @@ def tile_attention_pa_t_kernel(tc, hidden_states, freqs_cis, Wq, bq, Wk, bk, out
             tp_w = w_transposes(1, hh)
             w_copy(tp_w, 1, hh, nc.scalar.copy)
         fx(2)
+        for a in range(2):
+            nc.scalar.copy(out=f_dup[:, 4:8, a, :], in_=f_raw[:, 1].bitcast(F32))
         mx(0, 2)
         mx(0, 3)
         vmult(0, 1, 0, GROUP)
         gsum(0)
         quant_w(1, 0, 2)
-        table_dup(1)
         vmult(0, 2, 0, GROUP)
         vmult(0, 3, 0, GROUP)
         fx(3)

@@ -173,9 +173,12 @@ def tile_attention_pa_t_kernel(tc, hidden_states, freqs_cis, Wq, bq, Wk, bk, out
             nc.gpsimd.tensor_scalar(
                 out=nsc_tab[:, hf, 0, :], in0=cs_tab[:, hf, 1, :], scalar1=-1.0, scalar2=0.0, op0=MULT, op1=ADD
             )
-            nc.gpsimd.tensor_scalar(
-                out=nsc_tab[:, hf, 1, :], in0=cs_tab[:, hf, 0, :], scalar1=1.0, scalar2=0.0, op0=MULT, op1=ADD
-            )
+            if hf == 0:
+                nc.scalar.copy(out=nsc_tab[:, hf, 1, :], in_=cs_tab[:, hf, 0, :])
+            else:
+                nc.gpsimd.tensor_scalar(
+                    out=nsc_tab[:, hf, 1, :], in0=cs_tab[:, hf, 0, :], scalar1=1.0, scalar2=0.0, op0=MULT, op1=ADD
+                )
 
         acc = {}
         prod = {}

@@ -260,31 +260,28 @@ def tile_attention_pa_t_kernel(tc, hidden_states, freqs_cis, Wq, bq, Wk, bk, out
                 outs[t] = o_new
             o = outs[t]
             dst_rows = out_rows[qk][g * GROUP : (g + 1) * GROUP, :].rearrange("(p n) f -> p n f", n=4)
+            banks = []
             for n in n_list:
-                cols = slice(n * P, (n + 1) * P)
                 bt = psum.tile([P, D], F32, tag="tp", bufs=4, name="bt")
-                for hh in range(2):
-                    for ri in range(2):
-                        dst = bt[:, ri * 256 + hh * P : ri * 256 + (hh + 1) * P]
-                        if hh == 0 and t in sums:
-                            nc.tensor.transpose(dst, sums[t][:, ri, cols], ident[:])
-                        else:
-                            nc.tensor.matmul(
-                                out=dst,
-                                lhsT=prod[(t, 2 * hh)][:, ri, cols],
-                                rhs=ident[:],
-                                is_transpose=True,
-                                start=True,
-                                stop=False,
-                            )
-                            nc.tensor.matmul(
-                                out=dst,
-                                lhsT=prod[(t, 2 * hh + 1)][:, ri, cols],
-                                rhs=ident[:],
-                                is_transpose=True,
-                                start=False,
-                                stop=True,
-                            )
+                banks.append((slice(n * P, (n + 1) * P), bt))
+            for hh in range(2):
+                for ri in range(2):
+                    dst = slice(ri * 256 + hh * P, ri * 256 + (hh + 1) * P)
+                    if hh == 0 and t in sums:
+                        for cols, bt in banks:
+                            nc.tensor.transpose(bt[:, dst], sums[t][:, ri, cols], ident[:])
+                    else:
+                        for part in range(2):
+                            for cols, bt in banks:
+                                nc.tensor.matmul(
+                                    out=bt[:, dst],
+                                    lhsT=prod[(t, 2 * hh + part)][:, ri, cols],
+                                    rhs=ident[:],
+                                    is_transpose=True,
+                                    start=(part == 0),
+                                    stop=(part == 1),
+                                )
+            for n, (cols, bt) in zip(n_list, banks):
                 nc.scalar.copy(
                     out=o[:, n, :].rearrange("p (h ri j) -> p h ri j", h=4, ri=2),
                     in_=bt[:].rearrange("p (ri h j) -> p h ri j", ri=2, h=4),

@@ -340,11 +340,11 @@ def tile_attention_pa_t_kernel(tc, hidden_states, freqs_cis, Wq, bq, Wk, bk, out
             vmult(t, 2, 0, GROUP)
             if not side(t):
                 vmult(t, 3, 0, GROUP)
+            dummies(1, "tp", 4)
             if t + 4 < N_STEPS:
                 fx(t + 4)
             if t % 2 == 1 and t + 5 < N_STEPS:
                 split_x((t + 5) // 2)
-            dummies(1, "tp", 4)
             back(t - 1, (0, 1))
             banks_a(t + 1)
             back(t - 1, (2, 3))

@@ -264,7 +264,7 @@ def tile_attention_pa_t_kernel(tc, hidden_states, freqs_cis, Wq, bq, Wk, bk, out
             for n in n_list:
                 bt = psum.tile([P, D], F32, tag="tp", bufs=4, name="bt")
                 banks.append((slice(n * P, (n + 1) * P), bt))
-            for hh in range(2):
+            for hh in (1, 0):
                 for ri in range(2):
                     dst = slice(ri * 256 + hh * P, ri * 256 + (hh + 1) * P)
                     if hh == 0 and t in sums:

@@ -253,7 +253,7 @@ def tile_attention_pa_t_kernel(tc, hidden_states, freqs_cis, Wq, bq, Wk, bk, out
 
         outs = {}
 
-        def back(t, n_list):
+        def back(t, n_list, pair_order=(1, 0)):
             g, qk = divmod(t, 2)
             if t not in outs:
                 o_new = work.tile([P, 4, D], F32, tag="o", bufs=3, name="o")
@@ -264,7 +264,7 @@ def tile_attention_pa_t_kernel(tc, hidden_states, freqs_cis, Wq, bq, Wk, bk, out
             for n in n_list:
                 bt = psum.tile([P, D], F32, tag="tp", bufs=4, name="bt")
                 banks.append((slice(n * P, (n + 1) * P), bt))
-            for hh in (1, 0):
+            for hh in pair_order:
                 for ri in range(2):
                     dst = slice(ri * 256 + hh * P, ri * 256 + (hh + 1) * P)
                     if hh == 0 and t in sums:
@@ -355,9 +355,8 @@ def tile_attention_pa_t_kernel(tc, hidden_states, freqs_cis, Wq, bq, Wk, bk, out
             vmult(last, i, 0, half)
         back(last - 1, (0, 1))
         back(last - 1, (2, 3))
-        for i in range(4):
-            vmult(last, i, half, GROUP)
-        back(last, (0,))
-        back(last, (1,))
-        back(last, (2,))
-        back(last, (3,))
+        for n in (2, 3):
+            for i in range(4):
+                vmult(last, i, n * P, (n + 1) * P)
+        for n in range(4):
+            back(last, (n,), (0, 1))

@@ -231,6 +231,14 @@ def tile_attention_pa_t_kernel(tc, hidden_states, freqs_cis, Wq, bq, Wk, bk, out
             sums[t] = sm
             nc.gpsimd.tensor_tensor(out=sm[:], in0=prod[(t, 0)][:], in1=prod[(t, 1)][:], op=ADD)
 
+        def gsum_part(t, c0, c1):
+            if t not in sums:
+                sm_new = work.tile([P, 2, GROUP], F32, tag="sm", bufs=3, name="sm")
+                sums[t] = sm_new
+            nc.gpsimd.tensor_tensor(
+                out=sums[t][:, :, c0:c1], in0=prod[(t, 0)][:, :, c0:c1], in1=prod[(t, 1)][:, :, c0:c1], op=ADD
+            )
+
         def side(t):
             return t % 2 == 1 and 3 <= t < N_STEPS - 1
 
@@ -330,7 +338,7 @@ def tile_attention_pa_t_kernel(tc, hidden_states, freqs_cis, Wq, bq, Wk, bk, out
         banks_b(1)
 
         last = N_STEPS - 1
-        for t in range(1, last):
+        for t in range(1, last - 1):
             g, qk = divmod(t, 2)
             vmult(t, 0, 0, GROUP)
             vmult(t, 1, 0, GROUP)
@@ -351,9 +359,20 @@ def tile_attention_pa_t_kernel(tc, hidden_states, freqs_cis, Wq, bq, Wk, bk, out
             banks_b(t + 1)
 
         half = GROUP // 2
+        for c0 in (0, half):
+            vmult(last - 1, 0, c0, c0 + half)
+            vmult(last - 1, 1, c0, c0 + half)
+            gsum_part(last - 1, c0, c0 + half)
+            vmult(last - 1, 2, c0, c0 + half)
+            vmult(last - 1, 3, c0, c0 + half)
+        dummies(1, "tp", 4)
+        back(last - 2, (0, 1))
+        back(last - 2, (2, 3))
+        banks_a(last)
+        back(last - 1, (0, 1))
+        banks_b(last)
         for i in range(4):
             vmult(last, i, 0, half)
-        back(last - 1, (0, 1))
         back(last - 1, (2, 3))
         for n in (2, 3):
             for i in range(4):

@@ -261,7 +261,7 @@ def tile_attention_pa_t_kernel(tc, hidden_states, freqs_cis, Wq, bq, Wk, bk, out
 
         outs = {}
 
-        def back(t, n_list, pair_order=(1, 0)):
+        def back(t, n_list, pair_order=(1, 0), store_each=False):
             g, qk = divmod(t, 2)
             if t not in outs:
                 o_new = work.tile([P, 4, D], F32, tag="o", bufs=3, name="o")
@@ -294,10 +294,37 @@ def tile_attention_pa_t_kernel(tc, hidden_states, freqs_cis, Wq, bq, Wk, bk, out
                     out=o[:, n, :].rearrange("p (h ri j) -> p h ri j", h=4, ri=2),
                     in_=bt[:].rearrange("p (ri h j) -> p h ri j", ri=2, h=4),
                 )
-            n0 = n_list[0]
-            n1 = n_list[-1] + 1
-            nc.sync.dma_start(out=dst_rows[:, n0:n1, :], in_=o[:, n0:n1, :])
+                if store_each:
+                    nc.sync.dma_start(out=dst_rows[:, n, :], in_=o[:, n, :])
+            if not store_each:
+                n0 = n_list[0]
+                n1 = n_list[-1] + 1
+                nc.sync.dma_start(out=dst_rows[:, n0:n1, :], in_=o[:, n0:n1, :])
 
+
+        def back_by_pairs(t, n):
+            g, qk = divmod(t, 2)
+            o = outs[t]
+            dst_rows = out_rows[qk][g * GROUP : (g + 1) * GROUP, :].rearrange("(p n) f -> p n f", n=4)
+            cols = slice(n * P, (n + 1) * P)
+            for hh in range(2):
+                bt = psum.tile([P, D], F32, tag="tp", bufs=4, name="btp")
+                for ri in range(2):
+                    for part in range(2):
+                        nc.tensor.matmul(
+                            out=bt[:, ri * P : (ri + 1) * P],
+                            lhsT=prod[(t, 2 * hh + part)][:, ri, cols],
+                            rhs=ident[:],
+                            is_transpose=True,
+                            start=(part == 0),
+                            stop=(part == 1),
+                        )
+                feats = slice(hh * 2 * P, (hh + 1) * 2 * P)
+                nc.scalar.copy(
+                    out=o[:, n, feats].rearrange("p (h ri j) -> p h ri j", h=2, ri=2),
+                    in_=bt[:, 0 : 2 * P].rearrange("p (ri h j) -> p h ri j", ri=2, h=2),
+                )
+                nc.sync.dma_start(out=dst_rows[:, n, feats], in_=o[:, n, feats])
 
         fx(0)
         tp_w = w_transposes(0, 0)
@@ -369,13 +396,14 @@ def tile_attention_pa_t_kernel(tc, hidden_states, freqs_cis, Wq, bq, Wk, bk, out
         back(last - 2, (0, 1))
         back(last - 2, (2, 3))
         banks_a(last)
-        back(last - 1, (0, 1))
+        back(last - 1, (0, 1), (1, 0), True)
         banks_b(last)
         for i in range(4):
             vmult(last, i, 0, half)
-        back(last - 1, (2, 3))
+        back(last - 1, (2, 3), (1, 0), True)
         for n in (2, 3):
             for i in range(4):
                 vmult(last, i, n * P, (n + 1) * P)
-        for n in range(4):
+        for n in range(3):
             back(last, (n,), (0, 1))
+        back_by_pairs(last, 3)

@@ -69,17 +69,17 @@ def tile_attention_pa_t_kernel(tc, hidden_states, freqs_cis, Wq, bq, Wk, bk, out
 
         f_view = freqs_cis.rearrange("(hf p n) j c -> p hf n (j c)", hf=2, n=4)
 
-        with nc.allow_non_contiguous_dma(reason="each bias is 1 KiB, laid one feature pair to a partition"):
-            for qk in range(2):
-                nc.scalar.dma_start(
-                    out=b_raw[qk][:],
-                    in_=b_dram[qk].rearrange("(hh m eo) -> m hh eo", hh=2, eo=2),
-                )
         load_x(0, 0, 2)
         load_w(0, 0)
         load_x(0, 2, 4)
         load_w(0, 1)
         nc.sync.dma_start(out=f_raw[:, 0], in_=f_view[:, 0])
+        with nc.allow_non_contiguous_dma(reason="each bias is 1 KiB, laid one feature pair to a partition"):
+            for qk in range(2):
+                nc.sync.dma_start(
+                    out=b_raw[qk][:],
+                    in_=b_dram[qk].rearrange("(hh m eo) -> m hh eo", hh=2, eo=2),
+                )
         load_w(1, 0)
         load_w(1, 1)
         load_x(1, 0, 4)

@@ -72,8 +72,8 @@ def tile_attention_pa_t_kernel(tc, hidden_states, freqs_cis, Wq, bq, Wk, bk, out
         load_x(0, 0, 2)
         load_w(0, 0)
         load_x(0, 2, 4)
-        load_w(0, 1)
         nc.sync.dma_start(out=f_raw[:, 0], in_=f_view[:, 0])
+        load_w(0, 1)
         with nc.allow_non_contiguous_dma(reason="each bias is 1 KiB, laid one feature pair to a partition"):
             for qk in range(2):
                 nc.sync.dma_start(
@@ -164,12 +164,14 @@ def tile_attention_pa_t_kernel(tc, hidden_states, freqs_cis, Wq, bq, Wk, bk, out
             for a in range(2):
                 nc.vector.tensor_copy(out=f_dup[:, hf * 4 : (hf + 1) * 4, a, :], in_=words)
 
-        def table_make(hf):
+        def table_make(hf, w_half=None):
             tp = psum.tile([P, 4, P], F32, tag="tp", bufs=4, name="tpf")
             for n in range(4):
                 nc.tensor.transpose(tp[:, n, :], f_dup[:, hf * 4 + n].rearrange("p a j -> p (a j)"), ident[:])
             halves = tp[:].rearrange("p n r -> p (n r)").bitcast(BF16).rearrange("p (t c) -> p c t", c=2)
             nc.scalar.copy(out=cs_tab[:, hf], in_=halves)
+            if w_half is not None:
+                w_copy(w_transposes(0, w_half), 0, w_half, nc.scalar.copy)
             nc.gpsimd.tensor_scalar(
                 out=nsc_tab[:, hf, 0, :], in0=cs_tab[:, hf, 1, :], scalar1=-1.0, scalar2=0.0, op0=MULT, op1=ADD
             )
@@ -330,12 +332,10 @@ def tile_attention_pa_t_kernel(tc, hidden_states, freqs_cis, Wq, bq, Wk, bk, out
         tp_w = w_transposes(0, 0)
         w_copy(tp_w, 0, 0, nc.vector.tensor_copy)
         fx(1)
-        tp_w = w_transposes(0, 1)
         table_dup(0)
         quant_w(0, 0, 1)
-        table_make(0)
+        table_make(0, 1)
         quant_x(0)
-        w_copy(tp_w, 0, 1, nc.vector.tensor_copy)
         for qk in range(2):
             nc.vector.tensor_copy(
                 out=bias_f[:, qk * 4 : (qk + 1) * 4], in_=b_raw[qk][:].rearrange("p hh eo -> p (hh eo)")

@@ -375,7 +375,6 @@ def tile_attention_pa_t_kernel(tc, hidden_states, freqs_cis, Wq, bq, Wk, bk, out
             vmult(t, 2, 0, GROUP)
             if not side(t):
                 vmult(t, 3, 0, GROUP)
-            dummies(1, "tp", 4)
             if t + 4 < N_STEPS:
                 fx(t + 4)
             if t % 2 == 1 and t + 5 < N_STEPS:
@@ -392,7 +391,6 @@ def tile_attention_pa_t_kernel(tc, hidden_states, freqs_cis, Wq, bq, Wk, bk, out
             gsum_part(last - 1, c0, c0 + half)
             vmult(last - 1, 2, c0, c0 + half)
             vmult(last - 1, 3, c0, c0 + half)
-        dummies(1, "tp", 4)
         back(last - 2, (0, 1))
         back(last - 2, (2, 3))
         banks_a(last)

@@ -228,10 +228,38 @@ def tile_attention_pa_t_kernel(tc, hidden_states, freqs_cis, Wq, bq, Wk, bk, out
                 out=pr[:], in0=ob[:].unsqueeze(1).to_broadcast([P, 2, GROUP]), in1=nsc_tab[:, g % 2], op=MULT
             )
 
+        half_bias = {}
+        prod_half = {}
+
+        def shared(t):
+            return t % 2 == 0 and 2 <= t <= N_STEPS - 4
+
+        def shared_bias(t):
+            w = (t % 2) * 4 + 3
+            ob = work.tile([P, GROUP // 2], F32, tag="ob", bufs=2, name="obh")
+            half_bias[t] = ob
+            nc.scalar.activation(
+                out=ob[:], in_=acc[(t, 3)][:, GROUP // 2 : GROUP], func=IDENTITY, bias=bias_f[:, w : w + 1], scale=1.0
+            )
+
+        def shared_mult(t):
+            g = t // 2
+            pr = work.tile([P, 2, GROUP // 2], F32, tag="prg", bufs=3, name="prh")
+            prod_half[(t, 3)] = pr
+            nc.gpsimd.tensor_tensor(
+                out=pr[:],
+                in0=half_bias[t][:].unsqueeze(1).to_broadcast([P, 2, GROUP // 2]),
+                in1=nsc_tab[:, g % 2, :, GROUP // 2 : GROUP],
+                op=MULT,
+            )
+
         def gsum(t):
             sm = work.tile([P, 2, GROUP], F32, tag="sm", bufs=3, name="sm")
             sums[t] = sm
-            nc.gpsimd.tensor_tensor(out=sm[:], in0=prod[(t, 0)][:], in1=prod[(t, 1)][:], op=ADD)
+            if shared(t):
+                nc.gpsimd.tensor_tensor(out=sm[:, 0, :], in0=prod[(t, 0)][:, 0, :], in1=prod[(t, 1)][:, 0, :], op=ADD)
+            else:
+                nc.gpsimd.tensor_tensor(out=sm[:], in0=prod[(t, 0)][:], in1=prod[(t, 1)][:], op=ADD)
 
         def gsum_part(t, c0, c1):
             if t not in sums:
@@ -273,25 +301,31 @@ def tile_attention_pa_t_kernel(tc, hidden_states, freqs_cis, Wq, bq, Wk, bk, out
             banks = []
             for n in n_list:
                 bt = psum.tile([P, D], F32, tag="tp", bufs=4, name="bt")
-                banks.append((slice(n * P, (n + 1) * P), bt))
+                banks.append((n, bt))
+
+            def product(i, ri, n):
+                if n >= 2 and (t, i) in prod_half:
+                    return prod_half[(t, i)][:, ri, (n - 2) * P : (n - 1) * P]
+                return prod[(t, i)][:, ri, n * P : (n + 1) * P]
+
             for hh in pair_order:
-                for ri in range(2):
+                for ri in (1, 0) if shared(t) else (0, 1):
                     dst = slice(ri * 256 + hh * P, ri * 256 + (hh + 1) * P)
-                    if hh == 0 and t in sums:
-                        for cols, bt in banks:
-                            nc.tensor.transpose(bt[:, dst], sums[t][:, ri, cols], ident[:])
+                    if hh == 0 and t in sums and not (shared(t) and ri == 1):
+                        for n, bt in banks:
+                            nc.tensor.transpose(bt[:, dst], sums[t][:, ri, n * P : (n + 1) * P], ident[:])
                     else:
                         for part in range(2):
-                            for cols, bt in banks:
+                            for n, bt in banks:
                                 nc.tensor.matmul(
                                     out=bt[:, dst],
-                                    lhsT=prod[(t, 2 * hh + part)][:, ri, cols],
+                                    lhsT=product(2 * hh + part, ri, n),
                                     rhs=ident[:],
                                     is_transpose=True,
                                     start=(part == 0),
                                     stop=(part == 1),
                                 )
-            for n, (cols, bt) in zip(n_list, banks):
+            for n, bt in banks:
                 nc.scalar.copy(
                     out=o[:, n, :].rearrange("p (h ri j) -> p h ri j", h=4, ri=2),
                     in_=bt[:].rearrange("p (ri h j) -> p h ri j", ri=2, h=4),
@@ -372,8 +406,12 @@ def tile_attention_pa_t_kernel(tc, hidden_states, freqs_cis, Wq, bq, Wk, bk, out
             if qk == 0 and g + 1 < N_GROUPS:
                 quant_x(g + 1)
             gsum(t)
+            if shared(t):
+                shared_mult(t)
             vmult(t, 2, 0, GROUP)
-            if not side(t):
+            if shared(t):
+                vmult(t, 3, 0, GROUP // 2)
+            elif not side(t):
                 vmult(t, 3, 0, GROUP)
             if t + 4 < N_STEPS:
                 fx(t + 4)
@@ -383,6 +421,8 @@ def tile_attention_pa_t_kernel(tc, hidden_states, freqs_cis, Wq, bq, Wk, bk, out
             banks_a(t + 1)
             back(t - 1, (2, 3))
             banks_b(t + 1)
+            if shared(t + 1):
+                shared_bias(t + 1)
 
         half = GROUP // 2
         for c0 in (0, half):

@@ -257,7 +257,10 @@ def tile_attention_pa_t_kernel(tc, hidden_states, freqs_cis, Wq, bq, Wk, bk, out
             sm = work.tile([P, 2, GROUP], F32, tag="sm", bufs=3, name="sm")
             sums[t] = sm
             if shared(t):
-                nc.gpsimd.tensor_tensor(out=sm[:, 0, :], in0=prod[(t, 0)][:, 0, :], in1=prod[(t, 1)][:, 0, :], op=ADD)
+                first = slice(0, GROUP // 2)
+                nc.gpsimd.tensor_tensor(
+                    out=sm[:, :, first], in0=prod[(t, 0)][:, :, first], in1=prod[(t, 1)][:, :, first], op=ADD
+                )
             else:
                 nc.gpsimd.tensor_tensor(out=sm[:], in0=prod[(t, 0)][:], in1=prod[(t, 1)][:], op=ADD)
 
@@ -309,9 +312,9 @@ def tile_attention_pa_t_kernel(tc, hidden_states, freqs_cis, Wq, bq, Wk, bk, out
                 return prod[(t, i)][:, ri, n * P : (n + 1) * P]
 
             for hh in pair_order:
-                for ri in (1, 0) if shared(t) else (0, 1):
+                for ri in range(2):
                     dst = slice(ri * 256 + hh * P, ri * 256 + (hh + 1) * P)
-                    if hh == 0 and t in sums and not (shared(t) and ri == 1):
+                    if hh == 0 and t in sums and not (shared(t) and n_list[0] >= 2):
                         for n, bt in banks:
                             nc.tensor.transpose(bt[:, dst], sums[t][:, ri, n * P : (n + 1) * P], ident[:])
                     else:

from contextlib import ExitStack

import concourse.mybir as mybir
from concourse.masks import make_identity

F32 = mybir.dt.float32
BF16 = mybir.dt.bfloat16
U32 = mybir.dt.uint32
U8 = mybir.dt.uint8
FP8X4 = mybir.dt.float8_e5m2_x4
ADD = mybir.AluOpType.add
MULT = mybir.AluOpType.mult
IDENTITY = mybir.ActivationFunctionType.Identity

P = 128
D = 512
TOKENS = 4096
GROUP = 512
N_GROUPS = TOKENS // GROUP
N_STEPS = 2 * N_GROUPS
HEAD_DUMMIES = 4

FLOPS = 2 * TOKENS * D * 2 * D


def tile_attention_pa_t_kernel(tc, hidden_states, freqs_cis, Wq, bq, Wk, bk, out_0, out_1):
    nc = tc.nc
    x_rows = hidden_states.rearrange("b s k -> (b s) k")
    out_rows = (
        out_0.rearrange("b s h d -> (b s) (h d)"),
        out_1.rearrange("b s h d -> (b s) (h d)"),
    )
    w_dram = (Wq, Wk)
    b_dram = (bq, bk)

    with ExitStack() as ctx:
        const = ctx.enter_context(tc.tile_pool(name="const", bufs=1))
        work = ctx.enter_context(tc.tile_pool(name="work", bufs=2))
        psum = ctx.enter_context(tc.psum_pool(name="psum", bufs=1))
        ctx.enter_context(tc.manual_schedule())

        w_raw = [const.tile([P, 2, 2, D], BF16, name="w_raw%d" % qk) for qk in range(2)]
        b_raw = [const.tile([P, 2, 2], BF16, name="b_raw%d" % qk) for qk in range(2)]
        x_raw = [const.tile([P, 4, D], BF16, name="x_raw%d" % g) for g in range(N_GROUPS)]
        f_raw = const.tile([P, 2, 4, P], BF16, name="f_raw")
        f_dup = const.tile([P, 8, 2, 64], F32, name="f_dup")
        cs_tab = const.tile([P, 2, 2, GROUP], BF16, name="cs_tab")
        nsc_tab = const.tile([P, 2, 2, GROUP], F32, name="nsc_tab")
        w_grouped = [const.tile([P, 4 * D], BF16, name="w_grouped%d" % qk, align_bytes=64) for qk in range(2)]
        w_codes = const.tile([P, 2 * D], U32, name="w_codes", align_bytes=64)
        w_scales = const.tile([P, 2 * D], U8, name="w_scales", align_bytes=64)
        bias_f = const.tile([P, 8], F32, name="bias_f")
        ident = const.tile([P, P], F32, name="ident")
        zeros = const.tile([P, GROUP], BF16, name="zeros")
        warm_in = const.tile([P, 1], F32, name="warm_in")
        warm_out = const.tile([P, 1], F32, name="warm_out")

        def load_w(qk, hh):
            nc.sync.dma_start(
                out=w_raw[qk][:, hh],
                in_=w_dram[qk].rearrange("(hh m eo) k -> m hh eo k", hh=2, eo=2)[:, hh],
            )

        def load_x(g, n0, n1):
            nc.sync.dma_start(
                out=x_raw[g][:, n0:n1, :],
                in_=x_rows[g * GROUP : (g + 1) * GROUP, :].rearrange("(p n) k -> p n k", n=4)[:, n0:n1, :],
            )

        f_view = freqs_cis.rearrange("(hf p n) j c -> p hf n (j c)", hf=2, n=4)

        load_x(0, 0, 2)
        load_w(0, 0)
        load_x(0, 2, 4)
        nc.sync.dma_start(out=f_raw[:, 0], in_=f_view[:, 0])
        load_w(0, 1)
        with nc.allow_non_contiguous_dma(reason="each bias is 1 KiB, laid one feature pair to a partition"):
            for qk in range(2):
                nc.sync.dma_start(
                    out=b_raw[qk][:],
                    in_=b_dram[qk].rearrange("(hh m eo) -> m hh eo", hh=2, eo=2),
                )
        load_w(1, 0)
        load_w(1, 1)
        load_x(1, 0, 4)
        nc.sync.dma_start(out=f_raw[:, 1], in_=f_view[:, 1])
        for g in range(2, N_GROUPS):
            load_x(g, 0, 4)

        nc.vector.memset(zeros[:], 0.0)
        nc.vector.memset(warm_in[:], 0.0)
        nc.scalar.copy(out=warm_out[:], in_=warm_in[:])
        make_identity(nc, ident[:])

        def dummies(count, tag, bufs):
            scratch = psum.tile([P, GROUP], F32, tag=tag, bufs=bufs, name="scratch")
            for i in range(count):
                nc.tensor.matmul(out=scratch[:], lhsT=zeros[:, 0:P], rhs=zeros[:], start=True, stop=True)

        dummies(HEAD_DUMMIES, "mx", 4)

        def k_transposes(rows_pair):
            tp = psum.tile([P, 2, 2, P], F32, tag="tp", bufs=4, name="tp")
            for i in range(2):
                words = rows_pair[i].bitcast(F32)
                for u in range(2):
                    nc.tensor.transpose(tp[:, u, i, :], words[:, u : D // 2 : 2], ident[:])
            return tp

        def k_copy(tp, grouped_words, copy):
            copy(out=grouped_words, in_=tp[:].rearrange("p u i r -> p (i r) u"))

        def w_transposes(qk, hh):
            return k_transposes((w_raw[qk][:, hh, 0, :], w_raw[qk][:, hh, 1, :]))

        def w_copy(tp, qk, hh, copy):
            words = w_grouped[qk][:].bitcast(F32).rearrange("p (c u) -> p c u", u=2)
            k_copy(tp, words[:, hh * 256 : (hh + 1) * 256, :], copy)

        def quant_w(qk, hh0, hh1):
            nc.vector.quantize_mx(
                out=w_codes[:, qk * D + hh0 * 256 : qk * D + hh1 * 256].bitcast(FP8X4),
                scales=w_scales[:, qk * D + hh0 * 256 : qk * D + hh1 * 256],
                in_=w_grouped[qk][:, hh0 * 1024 : hh1 * 1024],
            )

        x_grouped = {}
        x_codes = {}
        x_scales = {}

        x_split = {}

        def split_x(g):
            xs_new = work.tile([P, 4, 2, P], F32, tag="xsp", bufs=3, name="xsp")
            x_split[g] = xs_new
            nc.scalar.copy(
                out=xs_new[:], in_=x_raw[g][:].rearrange("p n k -> p (n k)").bitcast(F32).rearrange("p (n w u) -> p n u w", n=4, u=2)
            )

        def fx(f):
            g, hf = divmod(f, 2)
            if hf == 0:
                xg = work.tile([P, 4 * GROUP], BF16, tag="xg", bufs=2, name="xg", align_bytes=64)
                x_grouped[g] = xg
            words = x_grouped[g][:].bitcast(F32).rearrange("p (c u) -> p c u", u=2)
            if g in x_split:
                tp = psum.tile([P, 2, 2, P], F32, tag="tp", bufs=4, name="tp")
                for i in range(2):
                    for u in range(2):
                        nc.tensor.transpose(tp[:, u, i, :], x_split[g][:, 2 * hf + i, u, :], ident[:])
            else:
                tp = k_transposes((x_raw[g][:, 2 * hf, :], x_raw[g][:, 2 * hf + 1, :]))
            k_copy(tp, words[:, hf * 256 : (hf + 1) * 256, :], nc.scalar.copy)

        def quant_x(g):
            xc = work.tile([P, GROUP], U32, tag="xc", bufs=3, name="xc", align_bytes=64)
            xs = work.tile([P, GROUP], U8, tag="xs", bufs=3, name="xs", align_bytes=64)
            x_codes[g] = xc
            x_scales[g] = xs
            nc.vector.quantize_mx(out=xc[:].bitcast(FP8X4), scales=xs[:], in_=x_grouped[g][:])

        def table_dup(hf):
            words = f_raw[:, hf].bitcast(F32)
            for a in range(2):
                nc.vector.tensor_copy(out=f_dup[:, hf * 4 : (hf + 1) * 4, a, :], in_=words)

        def table_make(hf, w_half=None):
            tp = psum.tile([P, 4, P], F32, tag="tp", bufs=4, name="tpf")
            for n in range(4):
                nc.tensor.transpose(tp[:, n, :], f_dup[:, hf * 4 + n].rearrange("p a j -> p (a j)"), ident[:])
            halves = tp[:].rearrange("p n r -> p (n r)").bitcast(BF16).rearrange("p (t c) -> p c t", c=2)
            nc.scalar.copy(out=cs_tab[:, hf], in_=halves)
            if w_half is not None:
                w_copy(w_transposes(0, w_half), 0, w_half, nc.scalar.copy)
            nc.gpsimd.tensor_scalar(
                out=nsc_tab[:, hf, 0, :], in0=cs_tab[:, hf, 1, :], scalar1=-1.0, scalar2=0.0, op0=MULT, op1=ADD
            )
            if hf == 0:
                nc.scalar.copy(out=nsc_tab[:, hf, 1, :], in_=cs_tab[:, hf, 0, :])
            else:
                nc.gpsimd.tensor_scalar(
                    out=nsc_tab[:, hf, 1, :], in0=cs_tab[:, hf, 0, :], scalar1=1.0, scalar2=0.0, op0=MULT, op1=ADD
                )

        acc = {}
        prod = {}
        sums = {}

        def mx(t, i):
            g, qk = divmod(t, 2)
            w = qk * 4 + i
            a = psum.tile([P, GROUP], F32, tag="mx", bufs=4, name="acc")
            acc[(t, i)] = a
            nc.tensor.matmul_mx(
                out=a[:],
                lhsT=w_codes[:, w * P : (w + 1) * P].bitcast(FP8X4),
                lhsT_scale=w_scales[:, w * P : (w + 1) * P],
                rhs=x_codes[g][:].bitcast(FP8X4),
                rhs_scale=x_scales[g][:],
                start=True,
                stop=True,
            )

        def vmult(t, i, c0, c1):
            g, qk = divmod(t, 2)
            w = qk * 4 + i
            table = cs_tab if i % 2 == 0 else nsc_tab
            if (t, i) not in prod:
                pr_new = work.tile([P, 2, GROUP], F32, tag="prv", bufs=10, name="prv")
                prod[(t, i)] = pr_new
            nc.vector.scalar_tensor_tensor(
                out=prod[(t, i)][:, :, c0:c1],
                in0=acc[(t, i)][:, c0:c1].unsqueeze(1).to_broadcast([P, 2, c1 - c0]),
                scalar=bias_f[:, w : w + 1],
                in1=table[:, g % 2, :, c0:c1],
                op0=ADD,
                op1=MULT,
            )

        def side_mult(t):
            g, qk = divmod(t, 2)
            w = qk * 4 + 3
            ob = work.tile([P, GROUP], F32, tag="ob", bufs=2, name="ob")
            nc.scalar.activation(out=ob[:], in_=acc[(t, 3)][:], func=IDENTITY, bias=bias_f[:, w : w + 1], scale=1.0)
            pr = work.tile([P, 2, GROUP], F32, tag="prg", bufs=3, name="prg")
            prod[(t, 3)] = pr
            nc.gpsimd.tensor_tensor(
                out=pr[:], in0=ob[:].unsqueeze(1).to_broadcast([P, 2, GROUP]), in1=nsc_tab[:, g % 2], op=MULT
            )

        half_bias = {}
        prod_half = {}

        def shared(t):
            return t % 2 == 0 and 2 <= t <= N_STEPS - 4

        def shared_bias(t):
            w = (t % 2) * 4 + 3
            ob = work.tile([P, GROUP // 2], F32, tag="ob", bufs=2, name="obh")
            half_bias[t] = ob
            nc.scalar.activation(
                out=ob[:], in_=acc[(t, 3)][:, GROUP // 2 : GROUP], func=IDENTITY, bias=bias_f[:, w : w + 1], scale=1.0
            )

        def shared_mult(t):
            g = t // 2
            pr = work.tile([P, 2, GROUP // 2], F32, tag="prg", bufs=3, name="prh")
            prod_half[(t, 3)] = pr
            nc.gpsimd.tensor_tensor(
                out=pr[:],
                in0=half_bias[t][:].unsqueeze(1).to_broadcast([P, 2, GROUP // 2]),
                in1=nsc_tab[:, g % 2, :, GROUP // 2 : GROUP],
                op=MULT,
            )

        def gsum(t):
            sm = work.tile([P, 2, GROUP], F32, tag="sm", bufs=3, name="sm")
            sums[t] = sm
            if shared(t):
                first = slice(0, GROUP // 2)
                nc.gpsimd.tensor_tensor(
                    out=sm[:, :, first], in0=prod[(t, 0)][:, :, first], in1=prod[(t, 1)][:, :, first], op=ADD
                )
            else:
                nc.gpsimd.tensor_tensor(out=sm[:], in0=prod[(t, 0)][:], in1=prod[(t, 1)][:], op=ADD)

        def gsum_part(t, c0, c1):
            if t not in sums:
                sm_new = work.tile([P, 2, GROUP], F32, tag="sm", bufs=3, name="sm")
                sums[t] = sm_new
            nc.gpsimd.tensor_tensor(
                out=sums[t][:, :, c0:c1], in0=prod[(t, 0)][:, :, c0:c1], in1=prod[(t, 1)][:, :, c0:c1], op=ADD
            )

        def side(t):
            return t % 2 == 1 and 3 <= t < N_STEPS - 1

        def banks_a(t):
            if side(t):
                mx(t, 3)
                mx(t, 0)
                side_mult(t)
            else:
                mx(t, 0)
                mx(t, 1)

        def banks_b(t):
            if side(t):
                mx(t, 1)
                mx(t, 2)
            else:
                mx(t, 2)
                mx(t, 3)

        outs = {}

        def back(t, n_list, pair_order=(1, 0), store_each=False):
            g, qk = divmod(t, 2)
            if t not in outs:
                o_new = work.tile([P, 4, D], F32, tag="o", bufs=3, name="o")
                outs[t] = o_new
            o = outs[t]
            dst_rows = out_rows[qk][g * GROUP : (g + 1) * GROUP, :].rearrange("(p n) f -> p n f", n=4)
            banks = []
            for n in n_list:
                bt = psum.tile([P, D], F32, tag="tp", bufs=4, name="bt")
                banks.append((n, bt))

            def product(i, ri, n):
                if n >= 2 and (t, i) in prod_half:
                    return prod_half[(t, i)][:, ri, (n - 2) * P : (n - 1) * P]
                return prod[(t, i)][:, ri, n * P : (n + 1) * P]

            for hh in pair_order:
                for ri in range(2):
                    dst = slice(ri * 256 + hh * P, ri * 256 + (hh + 1) * P)
                    if hh == 0 and t in sums and not (shared(t) and n_list[0] >= 2):
                        for n, bt in banks:
                            nc.tensor.transpose(bt[:, dst], sums[t][:, ri, n * P : (n + 1) * P], ident[:])
                    else:
                        for part in range(2):
                            for n, bt in banks:
                                nc.tensor.matmul(
                                    out=bt[:, dst],
                                    lhsT=product(2 * hh + part, ri, n),
                                    rhs=ident[:],
                                    is_transpose=True,
                                    start=(part == 0),
                                    stop=(part == 1),
                                )
            for n, bt in banks:
                nc.scalar.copy(
                    out=o[:, n, :].rearrange("p (h ri j) -> p h ri j", h=4, ri=2),
                    in_=bt[:].rearrange("p (ri h j) -> p h ri j", ri=2, h=4),
                )
                if store_each:
                    nc.sync.dma_start(out=dst_rows[:, n, :], in_=o[:, n, :])
            if not store_each:
                n0 = n_list[0]
                n1 = n_list[-1] + 1
                nc.sync.dma_start(out=dst_rows[:, n0:n1, :], in_=o[:, n0:n1, :])


        def back_by_pairs(t, n):
            g, qk = divmod(t, 2)
            o = outs[t]
            dst_rows = out_rows[qk][g * GROUP : (g + 1) * GROUP, :].rearrange("(p n) f -> p n f", n=4)
            cols = slice(n * P, (n + 1) * P)
            for hh in range(2):
                bt = psum.tile([P, D], F32, tag="tp", bufs=4, name="btp")
                for ri in range(2):
                    for part in range(2):
                        nc.tensor.matmul(
                            out=bt[:, ri * P : (ri + 1) * P],
                            lhsT=prod[(t, 2 * hh + part)][:, ri, cols],
                            rhs=ident[:],
                            is_transpose=True,
                            start=(part == 0),
                            stop=(part == 1),
                        )
                feats = slice(hh * 2 * P, (hh + 1) * 2 * P)
                nc.scalar.copy(
                    out=o[:, n, feats].rearrange("p (h ri j) -> p h ri j", h=2, ri=2),
                    in_=bt[:, 0 : 2 * P].rearrange("p (ri h j) -> p h ri j", ri=2, h=2),
                )
                nc.sync.dma_start(out=dst_rows[:, n, feats], in_=o[:, n, feats])

        fx(0)
        tp_w = w_transposes(0, 0)
        w_copy(tp_w, 0, 0, nc.vector.tensor_copy)
        fx(1)
        table_dup(0)
        quant_w(0, 0, 1)
        table_make(0, 1)
        quant_x(0)
        for qk in range(2):
            nc.vector.tensor_copy(
                out=bias_f[:, qk * 4 : (qk + 1) * 4], in_=b_raw[qk][:].rearrange("p hh eo -> p (hh eo)")
            )
        mx(0, 0)
        mx(0, 1)
        vmult(0, 0, 0, GROUP)
        quant_w(0, 1, 2)
        for hh in range(2):
            tp_w = w_transposes(1, hh)
            w_copy(tp_w, 1, hh, nc.scalar.copy)
        fx(2)
        for a in range(2):
            nc.scalar.copy(out=f_dup[:, 4:8, a, :], in_=f_raw[:, 1].bitcast(F32))
        mx(0, 2)
        mx(0, 3)
        vmult(0, 1, 0, GROUP)
        gsum(0)
        quant_w(1, 0, 2)
        vmult(0, 2, 0, GROUP)
        vmult(0, 3, 0, GROUP)
        fx(3)
        banks_a(1)
        table_make(1)
        quant_x(1)
        fx(4)
        banks_b(1)

        last = N_STEPS - 1
        for t in range(1, last - 1):
            g, qk = divmod(t, 2)
            vmult(t, 0, 0, GROUP)
            vmult(t, 1, 0, GROUP)
            if qk == 0 and g + 1 < N_GROUPS:
                quant_x(g + 1)
            gsum(t)
            if shared(t):
                shared_mult(t)
            vmult(t, 2, 0, GROUP)
            if shared(t):
                vmult(t, 3, 0, GROUP // 2)
            elif not side(t):
                vmult(t, 3, 0, GROUP)
            if t + 4 < N_STEPS:
                fx(t + 4)
            if t % 2 == 1 and t + 5 < N_STEPS:
                split_x((t + 5) // 2)
            back(t - 1, (0, 1))
            banks_a(t + 1)
            back(t - 1, (2, 3))
            banks_b(t + 1)
            if shared(t + 1):
                shared_bias(t + 1)

        half = GROUP // 2
        for c0 in (0, half):
            vmult(last - 1, 0, c0, c0 + half)
            vmult(last - 1, 1, c0, c0 + half)
            gsum_part(last - 1, c0, c0 + half)
            vmult(last - 1, 2, c0, c0 + half)
            vmult(last - 1, 3, c0, c0 + half)
        back(last - 2, (0, 1))
        back(last - 2, (2, 3))
        banks_a(last)
        back(last - 1, (0, 1), (1, 0), True)
        banks_b(last)
        for i in range(4):
            vmult(last, i, 0, half)
        back(last - 1, (2, 3), (1, 0), True)
        for n in (2, 3):
            for i in range(4):
                vmult(last, i, n * P, (n + 1) * P)
        for n in range(3):
            back(last, (n,), (0, 1))
        back_by_pairs(last, 3)
